import numpy as np
import ml_dtypes


def mxq(x, axis, fmt="e4m3"):
    dtype, down = {"e4m3": (ml_dtypes.float8_e4m3fn, 7), "e5m2": (ml_dtypes.float8_e5m2, 14)}[fmt]
    v = np.moveaxis(np.asarray(x, np.float32).astype(ml_dtypes.bfloat16).astype(np.float64), axis, -1)
    blocks = v.reshape(v.shape[:-1] + (-1, 32))
    amax = np.abs(blocks).max(-1, keepdims=True)
    byte = np.maximum(np.where(amax > 0, np.frexp(amax)[1] - 1 + 127, 0) - down, 1)
    scale = np.exp2(byte - 127.0)
    codes = (blocks / scale).astype(np.float32).astype(dtype).astype(np.float64)
    return np.moveaxis((codes * scale).reshape(v.shape), -1, axis)


WIDE = False


def mx_kscale(k):
    if not WIDE:
        return np.ones(k)
    levels = np.array([10, -10, 5, -5, 0])
    if k % 512:
        return np.exp2(np.random.permutation(np.resize(levels, k // 32))).repeat(32)
    a = np.empty((k // 512, 16))
    for p in range(k // 512):
        a[p, :8] = np.random.permutation(np.resize(levels, 8))
        for g in range(8):
            far = levels[np.abs(levels - a[p, g]) >= 10]
            a[p, g + 8] = far[np.random.randint(len(far))]
    return np.exp2(a.ravel()).repeat(32)


BF16 = ml_dtypes.bfloat16


def bf(x):
    return np.asarray(x, np.float32).astype(BF16)


def f64(x):
    return np.asarray(x).astype(np.float64)


B, H, FEAT, AUX, NS, FC, C = 1024, 1024, 128, 128, 2, 1024, 256
IN = FEAT + AUX + NS


def sigmoid(v):
    return 1.0 / (1.0 + np.exp(-v))


def setup_inputs():
    s = mx_kscale(H)
    s = s / s.max()
    col = np.concatenate([np.full(FEAT, 0.6 / np.sqrt(FEAT)), np.full(AUX, 0.6 / np.sqrt(AUX)), np.full(NS, 0.6 / np.sqrt(NS))])
    return {"x": bf(np.random.standard_normal((B, NS))),
            "feat": bf(np.random.standard_normal((B, FEAT))),
            "aux1": bf(np.random.standard_normal((B, AUX))),
            "h": bf(np.random.standard_normal((B, H)) * s),
            "w_ih": bf(np.random.standard_normal((3 * H, IN)) * col),
            "w_hh": bf(np.random.standard_normal((3 * H, H)) / np.sqrt(H) / s),
            "b_ih": bf(np.random.standard_normal(3 * H) * 0.3),
            "b_hh": bf(np.random.standard_normal(3 * H) * 0.3)}


def core(x, feat, aux1, h, w_ih, w_hh, b_ih, b_hh):
    hh, wi, xx = f64(h), f64(w_ih), f64(x)
    gi = f64(feat) @ wi[:, :FEAT].T + f64(aux1) @ wi[:, FEAT:FEAT + AUX].T
    for j in range(NS):
        gi = gi + xx[:, j:j + 1] * wi[:, FEAT + AUX + j][None, :]
    gi = gi + f64(b_ih)
    gh = (mxq(hh, 1, "e4m3") @ mxq(f64(w_hh), 1, "e4m3").T) + f64(b_hh)
    i_r, i_z, i_n = np.split(gi, 3, axis=1)
    h_r, h_z, h_n = np.split(gh, 3, axis=1)
    r = sigmoid(i_r + h_r)
    z = sigmoid(i_z + h_z)
    n = np.tanh(i_n + r * h_n)
    return (1.0 - z) * n + z * hh


def e4m3fn_bytes(y):
    return np.clip(np.asarray(y, np.float64), -448.0, 448.0).astype(np.float32).astype(ml_dtypes.float8_e4m3fn).view(np.uint8)


def reference(x, feat, aux1, h, w_ih, w_hh, b_ih, b_hh):
    out = core(x, feat, aux1, h, w_ih, w_hh, b_ih, b_hh)
    s = np.max(np.abs(out), axis=-1, keepdims=True) / 448.0
    return out, e4m3fn_bytes(out / s)

@@ -1,0 +1,463 @@
+from contextlib import ExitStack
+
+import concourse.mybir as mybir
+from concourse.masks import make_identity
+
+B, H, FEAT, AUX, NS = 1024, 1024, 128, 128, 2
+IN = FEAT + AUX + NS
+FLOPS = 2 * B * 3 * H * (H + IN)
+
+F32 = mybir.dt.float32
+BF16 = mybir.dt.bfloat16
+U32 = mybir.dt.uint32
+U8 = mybir.dt.uint8
+FP8X4 = mybir.dt.float8_e4m3fn_x4
+FP8 = mybir.dt.float8_e4m3fn
+ALU = mybir.AluOpType
+ACT = mybir.ActivationFunctionType
+AX = mybir.AxisListType
+
+P = 128
+BH = 512
+NJ = 8
+NQ = 2 * NJ
+R, Z, N = 0, 1, 2
+ACC_BANKS = 5
+TP_BANKS = 3
+SLOTS = ((R, 0), (R, 1), (Z, 0), (Z, 1), (R, 2), (N, 0), (N, 1), (N, 2))
+COL0 = (0, FEAT, IN - P)
+PREP = {"prep_a": 2, "prep_b": 0, "prep_c": 3}
+FIRST_EXTRA = 3
+FLIP_LAG = 1
+ORDER = (("add", 1), ("cast", 0), ("prep_b", 0), ("mm_r", 0), ("amax", 0), ("ev_r", 0), ("prep_a", 0), ("tanh", 2), ("quant", 0),
+         ("sig", 1), ("mm_z", 0), ("flip", 0), ("ev_z", 0), ("quant", 0), ("blend", 3), ("prep_c", 0), ("mm_n", 1), ("ev_n", 1))
+DRAIN = (
+    (("flip", 2, 0), ("blend", 12), ("sig_r", 14), ("add", 14), ("mm_r", 15), ("ev_r", 15), ("mm_z", 15), ("ev_z", 15),
+     ("mm_n", 14), ("tanh", 13), ("sig_r", 15), ("ev_n", 14), ("blend", 13), ("sig_z", 14), ("flip", 2, 1), ("mm_n", 15),
+     ("tanh", 14), ("ev_n", 15), ("add", 15), ("flip", 2, 2), ("flip", 2, 3), ("blend", 14))
+    + tuple(("flip_part", 3, il, t) for t in (0, 1) for il in range(4))
+    + (("tanh", 15), ("sig_z", 15), ("amax", 2, 0), ("amax", 2, 1), ("blend", 15), ("amax", 2, 2), ("amax", 2, 3))
+    + tuple(("flip_part", 3, il, 2) for il in range(4))
+    + tuple(item for il in range(4) for item in (("flip_part", 3, il, 3), ("flip_out", 3, il)))
+    + (("amax", 3, 0), ("amax", 3, 1), ("cast", 3, 1), ("amax", 3, 2), ("cast", 3, 0), ("amax", 3, 3), ("cast", 3, 3), ("cast", 3, 2))
+)
+CAST_ON_VECTOR = ((3, 0), (3, 2))
+DRAIN_ON_VECTOR = (("add", 14), ("blend", 14), ("blend", 15))
+
+
+def chunk(q):
+    return q // NJ, (q % NJ) // 4, q % 4
+
+
+def x_on_tensor(gate, q):
+    return gate == N or (gate == R and q >= NJ)
+
+
+def widx(gate, j):
+    return 2 * j + gate if gate != N else 2 * NJ + j
+
+
+def tile_wavernncell_pa_kernel(tc, x, feat, aux1, h, w_ih, w_hh, b_ih, b_hh, out_0, out_1):
+    nc = tc.nc
+    with ExitStack() as ctx:
+        keep = ctx.enter_context(tc.tile_pool(name="keep", bufs=1))
+        raw = ctx.enter_context(tc.tile_pool(name="raw", bufs=4))
+        work = ctx.enter_context(tc.tile_pool(name="work", bufs=2))
+        psum = ctx.enter_context(tc.psum_pool(name="psum", bufs=1))
+        ctx.enter_context(tc.manual_schedule())
+
+        ident_f = keep.tile([P, P], F32, name="ident_f")
+        ident_b = keep.tile([P, P], BF16, name="ident_b")
+        zero = keep.tile([P, 1], F32, name="zero")
+        warm = keep.tile([P, 1], F32, name="warm")
+        hG = keep.tile([P, 2 * B * 4], BF16, name="hG", align_bytes=64)
+        hC = keep.tile([P, 2, B], U32, name="hC", align_bytes=64)
+        hS = keep.tile([P, 2, B], U8, name="hS", align_bytes=64)
+        wC = keep.tile([P, 3 * NJ, 2 * P], U32, name="wC", align_bytes=64)
+        wS = keep.tile([P, 3 * NJ, 2 * P], U8, name="wS", align_bytes=64)
+        WiT = keep.tile([P, NJ, len(SLOTS), P], BF16, name="WiT")
+        fT = keep.tile([P, B], BF16, name="fT")
+        aT = keep.tile([P, B], BF16, name="aT")
+        xT = keep.tile([P, B], BF16, name="xT")
+        Xbc = keep.tile([P, B * NS], BF16, name="Xbc")
+        wih = keep.tile([P, 6, 4 * IN], BF16, name="wih")
+        Xpad = keep.tile([P, 8, P], BF16, name="Xpad")
+        fraw = keep.tile([P, 8, FEAT], BF16, name="fraw")
+        araw = keep.tile([P, 8, AUX], BF16, name="araw")
+        bi = keep.tile([P, 6, 4], BF16, name="bi")
+        bh = keep.tile([P, 6, 4], BF16, name="bh")
+        bsum = keep.tile([P, 6, 4], F32, name="bsum")
+        bif = keep.tile([P, 6, 4], F32, name="bif")
+        bhf = keep.tile([P, 6, 4], F32, name="bhf")
+        wxs = keep.tile([P, 6, 4, NS], F32, name="wxs")
+        am = keep.tile([P, 8, 2], F32, name="am")
+        sq = keep.tile([P, 8], F32, name="sq")
+        sc = keep.tile([P, 8], F32, name="sc")
+
+        hG32 = hG.bitcast(F32).rearrange("p (g m u) -> p g m u", g=2, u=2)
+        hGv = hG.rearrange("p (g m t) -> p g m t", g=2, t=4)
+        Xv = Xbc.rearrange("p (m j) -> p m j", j=NS)
+        wihv = wih.rearrange("p a (t k) -> p a t k", t=4)
+        vcopy = nc.vector.tensor_copy
+        scopy = nc.scalar.copy
+        live = {}
+
+        def load_h(i):
+            hr = raw.tile([P, H], BF16, name="hraw", tag="hraw", bufs=4)
+            nc.sync.dma_start(out=hr, in_=h[i * P:(i + 1) * P, :])
+            live[("hraw", i)] = hr
+
+        def load_w(gate, j):
+            g, t = divmod(j, 4)
+            r0 = gate * H + g * 512
+            wr = raw.tile([P, H], BF16, name="wraw", tag="wraw", bufs=10)
+            nc.sync.dma_start(out=wr, in_=w_hh[r0:r0 + 512, :].rearrange("(m t) k -> m t k", t=4)[:, t, :])
+            live[("wraw", gate, j)] = wr
+
+        def load_wih(a):
+            nc.sync.dma_start(out=wih[:, a, :], in_=w_ih[a * 512:(a + 1) * 512, :].rearrange("(m t) k -> m (t k)", t=4))
+
+        def conv_wx(a):
+            nc.vector.tensor_copy(out=wxs[:, a, :, :], in_=wihv[:, a, :, FEAT + AUX:IN])
+
+        def word_transposes(src):
+            words = src.bitcast(F32)
+            tp = psum.tile([P, 4 * P], F32, name="tp", tag="tp", bufs=TP_BANKS)
+            for c in range(2):
+                for u in range(2):
+                    col = (2 * c + u) * P
+                    nc.tensor.transpose(tp[:, col:col + P], words[:, 256 * c + u:256 * (c + 1):2], ident_f)
+            return tp.rearrange("p (c u m) -> p c m u", c=2, u=2)
+
+        def prep_h(i, copy):
+            copy(out=hG32[:, :, i * P:(i + 1) * P, :], in_=word_transposes(live[("hraw", i)]))
+
+        def quant_h(b):
+            for c in range(2):
+                col = c * 4 * B + b * 4 * BH
+                nc.vector.quantize_mx(out=hC[:, c, b * BH:(b + 1) * BH].bitcast(FP8X4), scales=hS[:, c, b * BH:(b + 1) * BH],
+                                      in_=hG[:, col:col + 4 * BH])
+
+        def prep_whh(gate, j, copy):
+            k = widx(gate, j)
+            if k % 2 == 0:
+                wg = work.tile([P, 2, 2 * P * 4], BF16, name="wg", tag="wg", bufs=3, align_bytes=64)
+                live[("wg", k // 2)] = wg
+            copy(out=live[("wg", k // 2)][:, k % 2, :].bitcast(F32).rearrange("p (c m u) -> p c m u", c=2, u=2),
+                 in_=word_transposes(live[("wraw", gate, j)]))
+
+        def quant_whh(pair):
+            nc.vector.quantize_mx(out=wC[:, 2 * pair:2 * pair + 2, :].rearrange("p a c -> p (a c)").bitcast(FP8X4),
+                                  scales=wS[:, 2 * pair:2 * pair + 2, :].rearrange("p a c -> p (a c)"),
+                                  in_=live[("wg", pair)].rearrange("p a c -> p (a c)"))
+
+        def prep_wih(j, lo, hi, copy):
+            g, t = divmod(j, 4)
+            tb = psum.tile([P, len(SLOTS), P], BF16, name="tb", tag="tp", bufs=TP_BANKS)
+            for s in range(lo, hi):
+                gate, v = SLOTS[s]
+                col = t * IN + COL0[v]
+                nc.tensor.transpose(tb[:, s, :], wih[:, 2 * gate + g, col:col + P], ident_b)
+            copy(out=WiT[:, j, lo:hi, :], in_=tb[:, lo:hi, :])
+
+        def prep_rows(src, dst, lo, hi, copy):
+            tb = psum.tile([P, 8, P], BF16, name="tb", tag="tp", bufs=TP_BANKS)
+            for i in range(lo, hi):
+                nc.tensor.transpose(tb[:, i, :], src[:, i, :], ident_b)
+            copy(out=dst.rearrange("p (i m) -> p i m", i=8)[:, lo:hi, :], in_=tb[:, lo:hi, :])
+
+        def mm_block(gate, q):
+            b, g, t = chunk(q)
+            j = 4 * g + t
+            bs = slice(b * BH, (b + 1) * BH)
+            last = 2 if x_on_tensor(gate, q) else 1
+            a_ps = psum.tile([P, BH], F32, name="a_ps", tag="acc", bufs=ACC_BANKS)
+            m_ps = psum.tile([P, BH], F32, name="m_ps", tag="acc", bufs=ACC_BANKS)
+            live[("a_ps", gate, q)] = a_ps
+            live[("m_ps", gate, q)] = m_ps
+
+            def plain(v):
+                nc.tensor.matmul(out=a_ps, lhsT=WiT[:, j, SLOTS.index((gate, v)), :], rhs=(fT, aT, xT)[v][:, bs],
+                                 start=(v == 0), stop=(v == last))
+
+            plain(0)
+            for c in range(2):
+                w = widx(gate, j)
+                nc.tensor.matmul_mx(out=m_ps, lhsT=wC[:, w, c * P:(c + 1) * P].bitcast(FP8X4),
+                                    lhsT_scale=wS[:, w, c * P:(c + 1) * P], rhs=hC[:, c, bs].bitcast(FP8X4),
+                                    rhs_scale=hS[:, c, bs], start=(c == 0), stop=(c == 1))
+            for v in range(1, last + 1):
+                plain(v)
+
+        def ev_gate(gate, q):
+            b, g, t = chunk(q)
+            bs = slice(b * BH, (b + 1) * BH)
+            if gate == R:
+                a_new = work.tile([P, 2, BH], F32, name="pre_a", tag="pre_a", bufs=2)
+                b_new = work.tile([P, 2, BH], F32, name="pre_b", tag="pre_b", bufs=2)
+                live[("pre_a", q)] = a_new
+                live[("pre_b", q)] = b_new
+            pre_a = live[("pre_a", q)][:, gate, :]
+            pre_b = live[("pre_b", q)][:, gate, :]
+            a_ps = live[("a_ps", gate, q)]
+            m_ps = live[("m_ps", gate, q)]
+            if x_on_tensor(gate, q):
+                nc.scalar.copy(out=pre_a, in_=a_ps)
+                nc.vector.tensor_tensor(out=pre_a, in0=pre_a, in1=m_ps, op=ALU.add)
+            else:
+                nc.vector.scalar_tensor_tensor(out=pre_b, in0=Xv[:, bs, 1], scalar=wxs[:, 2 * gate + g, t, 1:2], in1=m_ps,
+                                               op0=ALU.mult, op1=ALU.add)
+                nc.vector.scalar_tensor_tensor(out=pre_a, in0=Xv[:, bs, 0], scalar=wxs[:, 2 * gate + g, t, 0:1], in1=a_ps,
+                                               op0=ALU.mult, op1=ALU.add)
+
+        def add_rz(q, eng):
+            pre_a = live[("pre_a", q)]
+            pre_b = live[("pre_b", q)]
+            lo = 1 if x_on_tensor(R, q) else 0
+            eng.tensor_tensor(out=pre_a[:, lo:2, :], in0=pre_a[:, lo:2, :], in1=pre_b[:, lo:2, :], op=ALU.add)
+
+        def sig_gate(gate, q):
+            b, g, t = chunk(q)
+            if gate == R:
+                rz_new = work.tile([P, 2, BH], F32, name="rz", tag="rz", bufs=4)
+                live[("rz", q)] = rz_new
+            nc.scalar.activation(out=live[("rz", q)][:, gate, :], in_=live[("pre_a", q)][:, gate, :], func=ACT.Sigmoid,
+                                 bias=bsum[:, 2 * gate + g, t:t + 1], scale=1.0)
+
+        def ev_n(q):
+            b, g, t = chunk(q)
+            u = work.tile([P, BH], F32, name="u", tag="u", bufs=2)
+            live[("u", q)] = u
+            nc.vector.scalar_tensor_tensor(out=u, in0=live[("m_ps", N, q)], scalar=bhf[:, 4 + g, t:t + 1],
+                                           in1=live[("rz", q)][:, R, :], op0=ALU.add, op1=ALU.mult)
+            nc.vector.tensor_tensor(out=u, in0=u, in1=live[("a_ps", N, q)], op=ALU.add)
+
+        def tanh_n(q):
+            b, g, t = chunk(q)
+            if t == 0:
+                n_new = work.tile([P, 4, BH], F32, name="n_grp", tag="n_grp", bufs=2)
+                live[("n_grp", q // 4)] = n_new
+            nc.scalar.activation(out=live[("n_grp", q // 4)][:, t, :], in_=live[("u", q)], func=ACT.Tanh,
+                                 bias=bif[:, 4 + g, t:t + 1], scale=1.0)
+
+        def blend(q, eng):
+            b, g, t = chunk(q)
+            if t == 0:
+                e_new = work.tile([P, 4, BH], F32, name="e_grp", tag="e_grp", bufs=2)
+                live[("e_grp", q // 4)] = e_new
+            e = live[("e_grp", q // 4)][:, t, :]
+            eng.tensor_tensor(out=e, in0=hGv[:, g, b * BH:(b + 1) * BH, t], in1=live[("n_grp", q // 4)][:, t, :],
+                              op=ALU.subtract)
+            eng.tensor_tensor(out=e, in0=live[("rz", q)][:, Z, :], in1=e, op=ALU.mult)
+
+        def flip_part(k, il, t):
+            if t == 0:
+                fl_new = psum.tile([P, 4, P], F32, name="fl", tag="tp" if (k < 3 or il < TP_BANKS) else "acc",
+                                   bufs=TP_BANKS if (k < 3 or il < TP_BANKS) else ACC_BANKS)
+                live[("fl", k, il)] = fl_new
+            for step, src in enumerate((live[("n_grp", k)], live[("e_grp", k)])):
+                nc.tensor.matmul(out=live[("fl", k, il)][:, t, :], lhsT=src[:, t, il * P:(il + 1) * P], rhs=ident_f,
+                                 is_transpose=True, start=(step == 0), stop=(step == 1))
+
+        def flip_out(k, il):
+            g = k % 2
+            i = 4 * (k // 2) + il
+            if g == 0:
+                o_new = work.tile([P, H], F32, name="o_row", tag="o_row", bufs=4)
+                live[("o_row", i)] = o_new
+            dst = live[("o_row", i)][:, g * 512:(g + 1) * 512]
+            nc.scalar.copy(out=dst.rearrange("r (p t) -> r p t", t=4), in_=live[("fl", k, il)].rearrange("r t p -> r p t"))
+            nc.scalar.dma_start(out=out_0[i * P:(i + 1) * P, g * 512:(g + 1) * 512], in_=dst)
+
+        def flip(k, il):
+            for t in range(4):
+                flip_part(k, il, t)
+            flip_out(k, il)
+
+        def amax(k, il):
+            g = k % 2
+            i = 4 * (k // 2) + il
+            nc.vector.tensor_reduce(out=am[:, i, g:g + 1], in_=live[("o_row", i)][:, g * 512:(g + 1) * 512], axis=AX.X,
+                                    op=ALU.max, apply_absolute_value=True)
+            if g == 1:
+                nc.vector.tensor_scalar(out=sq[:, i:i + 1], in0=am[:, i, 0:1], scalar1=am[:, i, 1:2],
+                                        scalar2=1.0 / 448.0, op0=ALU.max, op1=ALU.mult)
+                nc.vector.reciprocal(out=sc[:, i:i + 1], in_=sq[:, i:i + 1])
+
+        def cast(k, il):
+            i = 4 * (k // 2) + il
+            if k % 2 == 1:
+                f8 = work.tile([P, H], FP8, name="f8", tag="f8", bufs=4)
+                if (k, il) in CAST_ON_VECTOR:
+                    nc.vector.tensor_scalar(out=f8, in0=live[("o_row", i)], scalar1=sc[:, i:i + 1], scalar2=None,
+                                            op0=ALU.mult, saturate=False)
+                else:
+                    nc.scalar.activation(out=f8, in_=live[("o_row", i)], func=ACT.Identity, scale=sc[:, i:i + 1],
+                                         bias=zero[:, 0:1], saturate=False)
+                nc.sync.dma_start(out=out_1[i * P:(i + 1) * P, :], in_=f8.bitcast(U8))
+
+        fsrc = feat.rearrange("(i m) k -> m i k", m=P)
+        asrc = aux1.rearrange("(i m) k -> m i k", m=P)
+        nc.vector.memset(zero, 0.0)
+        nc.scalar.activation(out=warm, in_=zero, func=ACT.Sigmoid)
+        nc.vector.memset(Xpad, 0.0)
+        make_identity(nc, ident_f)
+        make_identity(nc, ident_b)
+
+        for i in range(4):
+            load_h(i)
+        load_w(R, 0)
+        load_w(Z, 0)
+        nc.sync.dma_start(out=fraw[:, 0:4, :], in_=fsrc[:, 0:4, :])
+        nc.sync.dma_start(out=araw[:, 0:4, :], in_=asrc[:, 0:4, :])
+        load_wih(0)
+        load_wih(2)
+        nc.sync.dma_start(out=Xbc, in_=x.rearrange("m j -> (m j)").partition_broadcast(P))
+        load_w(N, 0)
+        load_wih(4)
+        nc.sync.dma_start(out=Xpad[:, :, P - NS:P], in_=x.rearrange("(i m) j -> m i j", m=P))
+        nc.sync.dma_start(out=bi, in_=b_ih.rearrange("(a m t) -> m a t", a=6, t=4))
+        nc.sync.dma_start(out=bh, in_=b_hh.rearrange("(a m t) -> m a t", a=6, t=4))
+        for j in range(1, 3):
+            for gate in (R, Z, N):
+                load_w(gate, j)
+            if j == 1:
+                nc.sync.dma_start(out=fraw[:, 4:8, :], in_=fsrc[:, 4:8, :])
+                nc.sync.dma_start(out=araw[:, 4:8, :], in_=asrc[:, 4:8, :])
+
+        for i in range(4):
+            prep_h(i, vcopy if i % 2 else scopy)
+        quant_h(0)
+        prep_whh(R, 0, scopy)
+        prep_whh(Z, 0, vcopy)
+        prep_rows(fraw, fT, 0, 4, scopy)
+        prep_rows(araw, aT, 0, 4, scopy)
+        quant_whh(0)
+        prep_wih(0, 0, 4, vcopy)
+        conv_wx(0)
+        conv_wx(2)
+
+        units = [("whh", N, 0), ("wih", 0, 4), ("x",)]
+        for j in range(1, NJ):
+            units.extend([("whh", R, j), ("whh", Z, j), ("wih", j, 0), ("whh", N, j)])
+            if j == 4:
+                units.extend([("f",), ("a",)])
+            if j >= 4:
+                units.append(("h", j))
+        queue = {"units": units, "quant": [], "wait": [], "flip": [], "amax": [], "cast": []}
+
+        def do_units(count, share):
+            for c, un in enumerate(queue["units"][:count]):
+                copy = vcopy if (share and c % 2) else scopy
+                if un[0] == "whh":
+                    prep_whh(un[1], un[2], copy)
+                    if widx(un[1], un[2]) % 2 == 1:
+                        queue["quant"].append(widx(un[1], un[2]) // 2)
+                elif un[0] == "wih":
+                    prep_wih(un[1], un[2], len(SLOTS), copy)
+                elif un[0] == "x":
+                    prep_rows(Xpad, xT, 0, 8, copy)
+                elif un[0] == "f":
+                    prep_rows(fraw, fT, 4, 8, copy)
+                elif un[0] == "a":
+                    prep_rows(araw, aT, 4, 8, copy)
+                else:
+                    prep_h(un[1], copy)
+                    if un[1] == 7:
+                        queue["quant"].append(-1)
+            queue["units"] = queue["units"][count:]
+
+        def do_quants():
+            for pair in queue["quant"]:
+                if pair >= 0:
+                    quant_whh(pair)
+                else:
+                    quant_h(1)
+            queue["quant"] = []
+
+        def move(src, dst, count, fn):
+            for un in queue[src][:count]:
+                fn(un[0], un[1])
+            if dst:
+                queue[dst] = queue[dst] + queue[src][:count]
+            queue[src] = queue[src][count:]
+
+        def prefetch(it):
+            if it + 3 < NJ:
+                for gate in (R, Z, N):
+                    load_w(gate, it + 3)
+            if it < 4:
+                load_h(4 + it)
+            if it == 0:
+                for gate in (R, Z, N):
+                    load_wih(2 * gate + 1)
+            if it == 1:
+                for gate in (R, Z, N):
+                    conv_wx(2 * gate + 1)
+
+        def chunk_stage(name, q):
+            eng = nc.vector if (name, q) in DRAIN_ON_VECTOR else nc.gpsimd
+            if name == "mm_r":
+                mm_block(R, q)
+            elif name == "mm_z":
+                mm_block(Z, q)
+            elif name == "mm_n":
+                mm_block(N, q)
+            elif name == "ev_r":
+                ev_gate(R, q)
+            elif name == "ev_z":
+                ev_gate(Z, q)
+            elif name == "add":
+                add_rz(q, eng)
+            elif name == "sig":
+                sig_gate(R, q)
+                sig_gate(Z, q)
+            elif name == "sig_r":
+                sig_gate(R, q)
+            elif name == "sig_z":
+                sig_gate(Z, q)
+            elif name == "ev_n":
+                ev_n(q)
+            elif name == "tanh":
+                tanh_n(q)
+            else:
+                blend(q, eng)
+
+        for it in range(NQ - 1):
+            for name, lag in ORDER:
+                if name == "quant":
+                    do_quants()
+                elif name in PREP:
+                    do_units(PREP[name] + (FIRST_EXTRA if it == 0 and name == "prep_b" else 0), it == 0)
+                    if it == 0 and name == "prep_b":
+                        conv_wx(4)
+                        nc.vector.tensor_tensor(out=bsum, in0=bi, in1=bh, op=ALU.add)
+                        nc.vector.tensor_copy(out=bif, in_=bi)
+                        nc.vector.tensor_copy(out=bhf, in_=bh)
+                elif name == "flip":
+                    queue["flip"] = queue["flip"] + [un for un in queue["wait"] if un[2] <= it]
+                    queue["wait"] = [un for un in queue["wait"] if un[2] > it]
+                    move("flip", "amax", 1 if it < NJ else 2, flip)
+                elif name == "amax":
+                    move("amax", "cast", 4, amax)
+                elif name == "cast":
+                    move("cast", "", 4, cast)
+                elif 0 <= it - lag:
+                    chunk_stage(name, it - lag)
+                    if name == "blend" and (it - lag) % 4 == 3:
+                        queue["wait"] = queue["wait"] + [((it - lag) // 4, il, it + FLIP_LAG) for il in range(4)]
+            prefetch(it)
+
+        for item in DRAIN:
+            if item[0] == "flip":
+                flip(item[1], item[2])
+            elif item[0] == "flip_part":
+                flip_part(item[1], item[2], item[3])
+            elif item[0] == "flip_out":
+                flip_out(item[1], item[2])
+            elif item[0] == "amax":
+                amax(item[1], item[2])
+            elif item[0] == "cast":
+                cast(item[1], item[2])
+            else:
+                chunk_stage(item[0], item[1])

@@ -79,7 +79,7 @@ def tile_wavernncell_pa_kernel(tc, x, feat, aux1, h, w_ih, w_hh, b_ih, b_hh, out
         fT = keep.tile([P, B], BF16, name="fT")
         aT = keep.tile([P, B], BF16, name="aT")
         xT = keep.tile([P, B], BF16, name="xT")
-        Xbc = keep.tile([P, B * NS], BF16, name="Xbc")
+        Xb = keep.tile([P, NS, B], BF16, name="Xb")
         wih = keep.tile([P, 6, 4 * IN], BF16, name="wih")
         Xpad = keep.tile([P, 8, P], BF16, name="Xpad")
         fraw = keep.tile([P, 8, FEAT], BF16, name="fraw")
@@ -96,7 +96,6 @@ def tile_wavernncell_pa_kernel(tc, x, feat, aux1, h, w_ih, w_hh, b_ih, b_hh, out
 
         hG32 = hG.bitcast(F32).rearrange("p (g m u) -> p g m u", g=2, u=2)
         hGv = hG.rearrange("p (g m t) -> p g m t", g=2, t=4)
-        Xv = Xbc.rearrange("p (m j) -> p m j", j=NS)
         wihv = wih.rearrange("p a (t k) -> p a t k", t=4)
         vcopy = nc.vector.tensor_copy
         scopy = nc.scalar.copy
@@ -166,6 +165,14 @@ def tile_wavernncell_pa_kernel(tc, x, feat, aux1, h, w_ih, w_hh, b_ih, b_hh, out
                 nc.tensor.transpose(tb[:, i, :], src[:, i, :], ident_b)
             copy(out=dst.rearrange("p (i m) -> p i m", i=8)[:, lo:hi, :], in_=tb[:, lo:hi, :])
 
+        def prep_xb(b, copy):
+            tb = psum.tile([P, NS, 4, P], BF16, name="tb", tag="tp", bufs=TP_BANKS)
+            for d in range(NS):
+                for i in range(4):
+                    col = P - NS + d
+                    nc.tensor.transpose(tb[:, d, i, :], Xpad[:, 4 * b + i, col:col + 1].to_broadcast([P, P]), ident_b)
+            copy(out=Xb[:, :, b * BH:(b + 1) * BH], in_=tb.rearrange("p d i m -> p d (i m)"))
+
         def mm_block(gate, q):
             b, g, t = chunk(q)
             j = 4 * g + t
@@ -205,9 +212,9 @@ def tile_wavernncell_pa_kernel(tc, x, feat, aux1, h, w_ih, w_hh, b_ih, b_hh, out
                 nc.scalar.copy(out=pre_a, in_=a_ps)
                 nc.vector.tensor_tensor(out=pre_a, in0=pre_a, in1=m_ps, op=ALU.add)
             else:
-                nc.vector.scalar_tensor_tensor(out=pre_b, in0=Xv[:, bs, 1], scalar=wxs[:, 2 * gate + g, t, 1:2], in1=m_ps,
+                nc.vector.scalar_tensor_tensor(out=pre_b, in0=Xb[:, 1, bs], scalar=wxs[:, 2 * gate + g, t, 1:2], in1=m_ps,
                                                op0=ALU.mult, op1=ALU.add)
-                nc.vector.scalar_tensor_tensor(out=pre_a, in0=Xv[:, bs, 0], scalar=wxs[:, 2 * gate + g, t, 0:1], in1=a_ps,
+                nc.vector.scalar_tensor_tensor(out=pre_a, in0=Xb[:, 0, bs], scalar=wxs[:, 2 * gate + g, t, 0:1], in1=a_ps,
                                                op0=ALU.mult, op1=ALU.add)
 
         def add_rz(q, eng):
@@ -304,6 +311,7 @@ def tile_wavernncell_pa_kernel(tc, x, feat, aux1, h, w_ih, w_hh, b_ih, b_hh, out
         make_identity(nc, ident_f)
         make_identity(nc, ident_b)
 
+        nc.scalar.dma_start(out=Xpad[:, :, P - NS:P], in_=x.rearrange("(i m) j -> m i j", m=P))
         for i in range(4):
             load_h(i)
         load_w(R, 0)
@@ -312,10 +320,8 @@ def tile_wavernncell_pa_kernel(tc, x, feat, aux1, h, w_ih, w_hh, b_ih, b_hh, out
         nc.sync.dma_start(out=araw[:, 0:4, :], in_=asrc[:, 0:4, :])
         load_wih(0)
         load_wih(2)
-        nc.sync.dma_start(out=Xbc, in_=x.rearrange("m j -> (m j)").partition_broadcast(P))
         load_w(N, 0)
         load_wih(4)
-        nc.sync.dma_start(out=Xpad[:, :, P - NS:P], in_=x.rearrange("(i m) j -> m i j", m=P))
         nc.sync.dma_start(out=bi, in_=b_ih.rearrange("(a m t) -> m a t", a=6, t=4))
         nc.sync.dma_start(out=bh, in_=b_hh.rearrange("(a m t) -> m a t", a=6, t=4))
         for j in range(1, 3):
@@ -334,6 +340,7 @@ def tile_wavernncell_pa_kernel(tc, x, feat, aux1, h, w_ih, w_hh, b_ih, b_hh, out
         prep_rows(araw, aT, 0, 4, scopy)
         quant_whh(0)
         prep_wih(0, 0, 4, vcopy)
+        prep_xb(0, scopy)
         conv_wx(0)
         conv_wx(2)
 
@@ -341,7 +348,7 @@ def tile_wavernncell_pa_kernel(tc, x, feat, aux1, h, w_ih, w_hh, b_ih, b_hh, out
         for j in range(1, NJ):
             units.extend([("whh", R, j), ("whh", Z, j), ("wih", j, 0), ("whh", N, j)])
             if j == 4:
-                units.extend([("f",), ("a",)])
+                units.extend([("f",), ("a",), ("xb",)])
             if j >= 4:
                 units.append(("h", j))
         queue = {"units": units, "quant": [], "wait": [], "flip": [], "amax": [], "cast": []}
@@ -361,6 +368,8 @@ def tile_wavernncell_pa_kernel(tc, x, feat, aux1, h, w_ih, w_hh, b_ih, b_hh, out
                     prep_rows(fraw, fT, 4, 8, copy)
                 elif un[0] == "a":
                     prep_rows(araw, aT, 4, 8, copy)
+                elif un[0] == "xb":
+                    prep_xb(1, copy)
                 else:
                     prep_h(un[1], copy)
                     if un[1] == 7:

@@ -29,6 +29,7 @@ COL0 = (0, FEAT, IN - P)
 PREP = {"prep_a": 2, "prep_b": 0, "prep_c": 3}
 FIRST_EXTRA = 3
 FLIP_LAG = 1
+HOIST = 2
 ORDER = (("add", 1), ("cast", 0), ("prep_b", 0), ("mm_r", 0), ("amax", 0), ("ev_r", 0), ("prep_a", 0), ("tanh", 2), ("quant", 0),
          ("sig", 1), ("mm_z", 0), ("flip", 0), ("ev_z", 0), ("quant", 0), ("blend", 3), ("prep_c", 0), ("mm_n", 1), ("ev_n", 1))
 DRAIN = (
@@ -173,49 +174,56 @@ def tile_wavernncell_pa_kernel(tc, x, feat, aux1, h, w_ih, w_hh, b_ih, b_hh, out
                     nc.tensor.transpose(tb[:, d, i, :], Xpad[:, 4 * b + i, col:col + 1].to_broadcast([P, P]), ident_b)
             copy(out=Xb[:, :, b * BH:(b + 1) * BH], in_=tb.rearrange("p d i m -> p d (i m)"))
 
-        def mm_block(gate, q):
+        def mm_block(gate, q, part="both"):
             b, g, t = chunk(q)
             j = 4 * g + t
             bs = slice(b * BH, (b + 1) * BH)
             last = 2 if x_on_tensor(gate, q) else 1
-            a_ps = psum.tile([P, BH], F32, name="a_ps", tag="acc", bufs=ACC_BANKS)
-            m_ps = psum.tile([P, BH], F32, name="m_ps", tag="acc", bufs=ACC_BANKS)
-            live[("a_ps", gate, q)] = a_ps
-            live[("m_ps", gate, q)] = m_ps
+            if part != "mx":
+                a_ps = psum.tile([P, BH], F32, name="a_ps", tag="acc", bufs=ACC_BANKS)
+                live[("a_ps", gate, q)] = a_ps
+            if part != "plain":
+                m_ps = psum.tile([P, BH], F32, name="m_ps", tag="acc", bufs=ACC_BANKS)
+                live[("m_ps", gate, q)] = m_ps
 
             def plain(v):
-                nc.tensor.matmul(out=a_ps, lhsT=WiT[:, j, SLOTS.index((gate, v)), :], rhs=(fT, aT, xT)[v][:, bs],
+                nc.tensor.matmul(out=live[("a_ps", gate, q)], lhsT=WiT[:, j, SLOTS.index((gate, v)), :], rhs=(fT, aT, xT)[v][:, bs],
                                  start=(v == 0), stop=(v == last))
 
-            plain(0)
-            for c in range(2):
-                w = widx(gate, j)
-                nc.tensor.matmul_mx(out=m_ps, lhsT=wC[:, w, c * P:(c + 1) * P].bitcast(FP8X4),
-                                    lhsT_scale=wS[:, w, c * P:(c + 1) * P], rhs=hC[:, c, bs].bitcast(FP8X4),
-                                    rhs_scale=hS[:, c, bs], start=(c == 0), stop=(c == 1))
-            for v in range(1, last + 1):
-                plain(v)
+            if part != "mx":
+                plain(0)
+            if part != "plain":
+                for c in range(2):
+                    w = widx(gate, j)
+                    nc.tensor.matmul_mx(out=live[("m_ps", gate, q)], lhsT=wC[:, w, c * P:(c + 1) * P].bitcast(FP8X4),
+                                        lhsT_scale=wS[:, w, c * P:(c + 1) * P], rhs=hC[:, c, bs].bitcast(FP8X4),
+                                        rhs_scale=hS[:, c, bs], start=(c == 0), stop=(c == 1))
+            if part != "mx":
+                for v in range(1, last + 1):
+                    plain(v)
 
-        def ev_gate(gate, q):
+        def ev_gate(gate, q, part="both"):
             b, g, t = chunk(q)
             bs = slice(b * BH, (b + 1) * BH)
-            if gate == R:
+            if gate == R and part != "mx":
                 a_new = work.tile([P, 2, BH], F32, name="pre_a", tag="pre_a", bufs=2)
-                b_new = work.tile([P, 2, BH], F32, name="pre_b", tag="pre_b", bufs=2)
                 live[("pre_a", q)] = a_new
+            if gate == R and part != "plain":
+                b_new = work.tile([P, 2, BH], F32, name="pre_b", tag="pre_b", bufs=2)
                 live[("pre_b", q)] = b_new
-            pre_a = live[("pre_a", q)][:, gate, :]
-            pre_b = live[("pre_b", q)][:, gate, :]
-            a_ps = live[("a_ps", gate, q)]
-            m_ps = live[("m_ps", gate, q)]
             if x_on_tensor(gate, q):
-                nc.scalar.copy(out=pre_a, in_=a_ps)
-                nc.vector.tensor_tensor(out=pre_a, in0=pre_a, in1=m_ps, op=ALU.add)
+                pre_a = live[("pre_a", q)][:, gate, :]
+                nc.scalar.copy(out=pre_a, in_=live[("a_ps", gate, q)])
+                nc.vector.tensor_tensor(out=pre_a, in0=pre_a, in1=live[("m_ps", gate, q)], op=ALU.add)
             else:
-                nc.vector.scalar_tensor_tensor(out=pre_b, in0=Xb[:, 1, bs], scalar=wxs[:, 2 * gate + g, t, 1:2], in1=m_ps,
-                                               op0=ALU.mult, op1=ALU.add)
-                nc.vector.scalar_tensor_tensor(out=pre_a, in0=Xb[:, 0, bs], scalar=wxs[:, 2 * gate + g, t, 0:1], in1=a_ps,
-                                               op0=ALU.mult, op1=ALU.add)
+                if part != "plain":
+                    nc.vector.scalar_tensor_tensor(out=live[("pre_b", q)][:, gate, :], in0=Xb[:, 1, bs],
+                                                   scalar=wxs[:, 2 * gate + g, t, 1:2], in1=live[("m_ps", gate, q)],
+                                                   op0=ALU.mult, op1=ALU.add)
+                if part != "mx":
+                    nc.vector.scalar_tensor_tensor(out=live[("pre_a", q)][:, gate, :], in0=Xb[:, 0, bs],
+                                                   scalar=wxs[:, 2 * gate + g, t, 0:1], in1=live[("a_ps", gate, q)],
+                                                   op0=ALU.mult, op1=ALU.add)
 
         def add_rz(q, eng):
             pre_a = live[("pre_a", q)]
@@ -308,18 +316,18 @@ def tile_wavernncell_pa_kernel(tc, x, feat, aux1, h, w_ih, w_hh, b_ih, b_hh, out
         nc.vector.memset(zero, 0.0)
         nc.scalar.activation(out=warm, in_=zero, func=ACT.Sigmoid)
         nc.vector.memset(Xpad, 0.0)
-        make_identity(nc, ident_f)
         make_identity(nc, ident_b)
+        make_identity(nc, ident_f)
 
         nc.scalar.dma_start(out=Xpad[:, :, P - NS:P], in_=x.rearrange("(i m) j -> m i j", m=P))
-        for i in range(4):
-            load_h(i)
-        load_w(R, 0)
-        load_w(Z, 0)
         nc.sync.dma_start(out=fraw[:, 0:4, :], in_=fsrc[:, 0:4, :])
         nc.sync.dma_start(out=araw[:, 0:4, :], in_=asrc[:, 0:4, :])
         load_wih(0)
         load_wih(2)
+        for i in range(4):
+            load_h(i)
+        load_w(R, 0)
+        load_w(Z, 0)
         load_w(N, 0)
         load_wih(4)
         nc.sync.dma_start(out=bi, in_=b_ih.rearrange("(a m t) -> m a t", a=6, t=4))
@@ -331,22 +339,25 @@ def tile_wavernncell_pa_kernel(tc, x, feat, aux1, h, w_ih, w_hh, b_ih, b_hh, out
                 nc.sync.dma_start(out=fraw[:, 4:8, :], in_=fsrc[:, 4:8, :])
                 nc.sync.dma_start(out=araw[:, 4:8, :], in_=asrc[:, 4:8, :])
 
-        for i in range(4):
-            prep_h(i, vcopy if i % 2 else scopy)
-        quant_h(0)
-        prep_whh(R, 0, scopy)
-        prep_whh(Z, 0, vcopy)
         prep_rows(fraw, fT, 0, 4, scopy)
-        prep_rows(araw, aT, 0, 4, scopy)
-        quant_whh(0)
-        prep_wih(0, 0, 4, vcopy)
-        prep_xb(0, scopy)
+        prep_rows(araw, aT, 0, 4, vcopy)
+        for q in range(HOIST):
+            prep_wih(q, 0, 4, scopy)
+        prep_xb(0, vcopy)
         conv_wx(0)
         conv_wx(2)
+        for i in range(4):
+            prep_h(i, scopy)
+            mm_block((R, Z)[i % 2], i // 2, "plain")
+            ev_gate((R, Z)[i % 2], i // 2, "plain")
+        quant_h(0)
+        prep_whh(R, 0, scopy)
+        prep_whh(Z, 0, scopy)
+        quant_whh(0)
 
         units = [("whh", N, 0), ("wih", 0, 4), ("x",)]
         for j in range(1, NJ):
-            units.extend([("whh", R, j), ("whh", Z, j), ("wih", j, 0), ("whh", N, j)])
+            units.extend([("whh", R, j), ("whh", Z, j), ("wih", j, 4 if j < HOIST else 0), ("whh", N, j)])
             if j == 4:
                 units.extend([("f",), ("a",), ("xb",)])
             if j >= 4:
@@ -406,16 +417,17 @@ def tile_wavernncell_pa_kernel(tc, x, feat, aux1, h, w_ih, w_hh, b_ih, b_hh, out
 
         def chunk_stage(name, q):
             eng = nc.vector if (name, q) in DRAIN_ON_VECTOR else nc.gpsimd
+            part = "mx" if q < HOIST else "both"
             if name == "mm_r":
-                mm_block(R, q)
+                mm_block(R, q, part)
             elif name == "mm_z":
-                mm_block(Z, q)
+                mm_block(Z, q, part)
             elif name == "mm_n":
                 mm_block(N, q)
             elif name == "ev_r":
-                ev_gate(R, q)
+                ev_gate(R, q, part)
             elif name == "ev_z":
-                ev_gate(Z, q)
+                ev_gate(Z, q, part)
             elif name == "add":
                 add_rz(q, eng)
             elif name == "sig":

@@ -31,9 +31,9 @@ FIRST_EXTRA = 3
 FLIP_LAG = 1
 HOIST = 2
 ORDER = (("add", 1), ("cast", 0), ("prep_b", 0), ("mm_r", 0), ("amax", 0), ("ev_r", 0), ("prep_a", 0), ("tanh", 2), ("quant", 0),
-         ("sig", 1), ("mm_z", 0), ("flip", 0), ("ev_z", 0), ("quant", 0), ("blend", 3), ("prep_c", 0), ("mm_n", 1), ("ev_n", 1))
+         ("sig", 1), ("mm_z", 0), ("flip", 0), ("ev_z", 0), ("quant", 0), ("mult", 3), ("sub", 2), ("prep_c", 0), ("mm_n", 1), ("ev_n", 1))
 DRAIN = (
-    (("flip", 2, 0), ("blend", 12), ("sig_r", 14), ("add", 14), ("mm_r", 15), ("ev_r", 15), ("mm_z", 15), ("ev_z", 15),
+    (("flip", 2, 0), ("mult", 12), ("sig_r", 14), ("add", 14), ("mm_r", 15), ("ev_r", 15), ("mm_z", 15), ("ev_z", 15),
      ("mm_n", 14), ("tanh", 13), ("sig_r", 15), ("ev_n", 14), ("blend", 13), ("sig_z", 14), ("flip", 2, 1), ("mm_n", 15),
      ("tanh", 14), ("ev_n", 15), ("add", 15), ("flip", 2, 2), ("flip", 2, 3), ("blend", 14))
     + tuple(("flip_part", 3, il, t) for t in (0, 1) for il in range(4))
@@ -228,8 +228,8 @@ def tile_wavernncell_pa_kernel(tc, x, feat, aux1, h, w_ih, w_hh, b_ih, b_hh, out
         def add_rz(q, eng):
             pre_a = live[("pre_a", q)]
             pre_b = live[("pre_b", q)]
-            lo = 1 if x_on_tensor(R, q) else 0
-            eng.tensor_tensor(out=pre_a[:, lo:2, :], in0=pre_a[:, lo:2, :], in1=pre_b[:, lo:2, :], op=ALU.add)
+            for gate in ((Z,) if x_on_tensor(R, q) else (R, Z)):
+                eng.tensor_tensor(out=pre_a[:, gate, :], in0=pre_a[:, gate, :], in1=pre_b[:, gate, :], op=ALU.add)
 
         def sig_gate(gate, q):
             b, g, t = chunk(q)
@@ -255,14 +255,16 @@ def tile_wavernncell_pa_kernel(tc, x, feat, aux1, h, w_ih, w_hh, b_ih, b_hh, out
             nc.scalar.activation(out=live[("n_grp", q // 4)][:, t, :], in_=live[("u", q)], func=ACT.Tanh,
                                  bias=bif[:, 4 + g, t:t + 1], scale=1.0)
 
-        def blend(q, eng):
+        def blend_sub(q, eng):
             b, g, t = chunk(q)
             if t == 0:
                 e_new = work.tile([P, 4, BH], F32, name="e_grp", tag="e_grp", bufs=2)
                 live[("e_grp", q // 4)] = e_new
-            e = live[("e_grp", q // 4)][:, t, :]
-            eng.tensor_tensor(out=e, in0=hGv[:, g, b * BH:(b + 1) * BH, t], in1=live[("n_grp", q // 4)][:, t, :],
-                              op=ALU.subtract)
+            eng.tensor_tensor(out=live[("e_grp", q // 4)][:, t, :], in0=hGv[:, g, b * BH:(b + 1) * BH, t],
+                              in1=live[("n_grp", q // 4)][:, t, :], op=ALU.subtract)
+
+        def blend_mult(q, eng):
+            e = live[("e_grp", q // 4)][:, q % 4, :]
             eng.tensor_tensor(out=e, in0=live[("rz", q)][:, Z, :], in1=e, op=ALU.mult)
 
         def flip_part(k, il, t):
@@ -441,8 +443,13 @@ def tile_wavernncell_pa_kernel(tc, x, feat, aux1, h, w_ih, w_hh, b_ih, b_hh, out
                 ev_n(q)
             elif name == "tanh":
                 tanh_n(q)
+            elif name == "sub":
+                blend_sub(q, eng)
+            elif name == "mult":
+                blend_mult(q, eng)
             else:
-                blend(q, eng)
+                blend_sub(q, eng)
+                blend_mult(q, eng)
 
         for it in range(NQ - 1):
             for name, lag in ORDER:
@@ -465,7 +472,7 @@ def tile_wavernncell_pa_kernel(tc, x, feat, aux1, h, w_ih, w_hh, b_ih, b_hh, out
                     move("cast", "", 4, cast)
                 elif 0 <= it - lag:
                     chunk_stage(name, it - lag)
-                    if name == "blend" and (it - lag) % 4 == 3:
+                    if name == "mult" and (it - lag) % 4 == 3:
                         queue["wait"] = queue["wait"] + [((it - lag) // 4, il, it + FLIP_LAG) for il in range(4)]
             prefetch(it)
 

@@ -85,8 +85,8 @@ def tile_wavernncell_pa_kernel(tc, x, feat, aux1, h, w_ih, w_hh, b_ih, b_hh, out
         Xpad = keep.tile([P, 8, P], BF16, name="Xpad")
         fraw = keep.tile([P, 8, FEAT], BF16, name="fraw")
         araw = keep.tile([P, 8, AUX], BF16, name="araw")
-        bi = keep.tile([P, 6, 4], BF16, name="bi")
-        bh = keep.tile([P, 6, 4], BF16, name="bh")
+        xraw = keep.tile([P, NS * P], BF16, name="xraw")
+        braw = keep.tile([P, 4 * P], BF16, name="braw")
         bsum = keep.tile([P, 6, 4], F32, name="bsum")
         bif = keep.tile([P, 6, 4], F32, name="bif")
         bhf = keep.tile([P, 6, 4], F32, name="bhf")
@@ -173,6 +173,13 @@ def tile_wavernncell_pa_kernel(tc, x, feat, aux1, h, w_ih, w_hh, b_ih, b_hh, out
                     col = P - NS + d
                     nc.tensor.transpose(tb[:, d, i, :], Xpad[:, 4 * b + i, col:col + 1].to_broadcast([P, P]), ident_b)
             copy(out=Xb[:, :, b * BH:(b + 1) * BH], in_=tb.rearrange("p d i m -> p d (i m)"))
+
+        def prep_small(rows, step, outs):
+            tb = psum.tile([P, 8, P], BF16, name="tb", tag="tp", bufs=TP_BANKS)
+            for s in range(step):
+                nc.tensor.transpose(tb[:, s, :], rows[:, s:step * P:step], ident_b)
+            for dst, lo, hi in outs:
+                nc.vector.tensor_copy(out=dst, in_=tb[:, 0:step, lo:hi].rearrange("p s r -> p r s"))
 
         def mm_block(gate, q, part="both"):
             b, g, t = chunk(q)
@@ -317,11 +324,13 @@ def tile_wavernncell_pa_kernel(tc, x, feat, aux1, h, w_ih, w_hh, b_ih, b_hh, out
         asrc = aux1.rearrange("(i m) k -> m i k", m=P)
         nc.vector.memset(zero, 0.0)
         nc.scalar.activation(out=warm, in_=zero, func=ACT.Sigmoid)
+        nc.vector.memset(xraw, 0.0)
         nc.vector.memset(Xpad, 0.0)
+        nc.vector.memset(braw, 0.0)
         make_identity(nc, ident_b)
         make_identity(nc, ident_f)
 
-        nc.scalar.dma_start(out=Xpad[:, :, P - NS:P], in_=x.rearrange("(i m) j -> m i j", m=P))
+        nc.scalar.dma_start(out=xraw[0:8, :], in_=x.rearrange("(i m) j -> i (m j)", m=P))
         nc.sync.dma_start(out=fraw[:, 0:4, :], in_=fsrc[:, 0:4, :])
         nc.sync.dma_start(out=araw[:, 0:4, :], in_=asrc[:, 0:4, :])
         load_wih(0)
@@ -332,8 +341,8 @@ def tile_wavernncell_pa_kernel(tc, x, feat, aux1, h, w_ih, w_hh, b_ih, b_hh, out
         load_w(Z, 0)
         load_w(N, 0)
         load_wih(4)
-        nc.sync.dma_start(out=bi, in_=b_ih.rearrange("(a m t) -> m a t", a=6, t=4))
-        nc.sync.dma_start(out=bh, in_=b_hh.rearrange("(a m t) -> m a t", a=6, t=4))
+        nc.sync.dma_start(out=braw[0:6, :], in_=b_ih.rearrange("(a c) -> a c", a=6))
+        nc.sync.dma_start(out=braw[6:12, :], in_=b_hh.rearrange("(a c) -> a c", a=6))
         for j in range(1, 3):
             for gate in (R, Z, N):
                 load_w(gate, j)
@@ -341,6 +350,7 @@ def tile_wavernncell_pa_kernel(tc, x, feat, aux1, h, w_ih, w_hh, b_ih, b_hh, out
                 nc.sync.dma_start(out=fraw[:, 4:8, :], in_=fsrc[:, 4:8, :])
                 nc.sync.dma_start(out=araw[:, 4:8, :], in_=asrc[:, 4:8, :])
 
+        prep_small(xraw, NS, [(Xpad[:, :, P - NS:P], 0, 8)])
         prep_rows(fraw, fT, 0, 4, scopy)
         prep_rows(araw, aT, 0, 4, vcopy)
         for q in range(HOIST):
@@ -459,9 +469,8 @@ def tile_wavernncell_pa_kernel(tc, x, feat, aux1, h, w_ih, w_hh, b_ih, b_hh, out
                     do_units(PREP[name] + (FIRST_EXTRA if it == 0 and name == "prep_b" else 0), it == 0)
                     if it == 0 and name == "prep_b":
                         conv_wx(4)
-                        nc.vector.tensor_tensor(out=bsum, in0=bi, in1=bh, op=ALU.add)
-                        nc.vector.tensor_copy(out=bif, in_=bi)
-                        nc.vector.tensor_copy(out=bhf, in_=bh)
+                        prep_small(braw, 4, [(bif, 0, 6), (bhf, 6, 12)])
+                        nc.vector.tensor_tensor(out=bsum, in0=bif, in1=bhf, op=ALU.add)
                 elif name == "flip":
                     queue["flip"] = queue["flip"] + [un for un in queue["wait"] if un[2] <= it]
                     queue["wait"] = [un for un in queue["wait"] if un[2] > it]

@@ -322,15 +322,15 @@ def tile_wavernncell_pa_kernel(tc, x, feat, aux1, h, w_ih, w_hh, b_ih, b_hh, out
 
         fsrc = feat.rearrange("(i m) k -> m i k", m=P)
         asrc = aux1.rearrange("(i m) k -> m i k", m=P)
+        nc.vector.memset(xraw, 0.0)
+        nc.scalar.dma_start(out=xraw[0:8, :], in_=x.rearrange("(i m) j -> i (m j)", m=P))
         nc.vector.memset(zero, 0.0)
         nc.scalar.activation(out=warm, in_=zero, func=ACT.Sigmoid)
-        nc.vector.memset(xraw, 0.0)
         nc.vector.memset(Xpad, 0.0)
         nc.vector.memset(braw, 0.0)
         make_identity(nc, ident_b)
         make_identity(nc, ident_f)
 
-        nc.scalar.dma_start(out=xraw[0:8, :], in_=x.rearrange("(i m) j -> i (m j)", m=P))
         nc.sync.dma_start(out=fraw[:, 0:4, :], in_=fsrc[:, 0:4, :])
         nc.sync.dma_start(out=araw[:, 0:4, :], in_=asrc[:, 0:4, :])
         load_wih(0)
@@ -350,11 +350,11 @@ def tile_wavernncell_pa_kernel(tc, x, feat, aux1, h, w_ih, w_hh, b_ih, b_hh, out
                 nc.sync.dma_start(out=fraw[:, 4:8, :], in_=fsrc[:, 4:8, :])
                 nc.sync.dma_start(out=araw[:, 4:8, :], in_=asrc[:, 4:8, :])
 
-        prep_small(xraw, NS, [(Xpad[:, :, P - NS:P], 0, 8)])
         prep_rows(fraw, fT, 0, 4, scopy)
         prep_rows(araw, aT, 0, 4, vcopy)
         for q in range(HOIST):
             prep_wih(q, 0, 4, scopy)
+        prep_small(xraw, NS, [(Xpad[:, :, P - NS:P], 0, 8)])
         prep_xb(0, vcopy)
         conv_wx(0)
         conv_wx(2)

@@ -19,8 +19,11 @@ AX = mybir.AxisListType
 
 P = 128
 BH = 512
+GROUPS = ((0, 512, 0), (0, 512, 1), (512, 512, 0), (512, 256, 1), (768, 256, 1))
 NJ = 8
-NQ = 2 * NJ
+NQ = 4 * len(GROUPS)
+LAST = NQ - 1
+KL = len(GROUPS) - 1
 R, Z, N = 0, 1, 2
 ACC_BANKS = 5
 TP_BANKS = 3
@@ -33,21 +36,31 @@ HOIST = 2
 ORDER = (("add", 1), ("cast", 0), ("prep_b", 0), ("mm_r", 0), ("amax", 0), ("ev_r", 0), ("prep_a", 0), ("tanh", 2), ("quant", 0),
          ("sig", 1), ("mm_z", 0), ("flip", 0), ("ev_z", 0), ("quant", 0), ("mult", 3), ("sub", 2), ("prep_c", 0), ("mm_n", 1), ("ev_n", 1))
 DRAIN = (
-    (("flip", 2, 0), ("mult", 12), ("sig_r", 14), ("add", 14), ("mm_r", 15), ("ev_r", 15), ("mm_z", 15), ("ev_z", 15),
-     ("mm_n", 14), ("tanh", 13), ("sig_r", 15), ("ev_n", 14), ("blend", 13), ("sig_z", 14), ("flip", 2, 1), ("mm_n", 15),
-     ("tanh", 14), ("ev_n", 15), ("add", 15), ("flip", 2, 2), ("flip", 2, 3), ("blend", 14))
-    + tuple(("flip_part", 3, il, t) for t in (0, 1) for il in range(4))
-    + (("tanh", 15), ("sig_z", 15), ("amax", 2, 0), ("amax", 2, 1), ("blend", 15), ("amax", 2, 2), ("amax", 2, 3))
-    + tuple(("flip_part", 3, il, 2) for il in range(4))
-    + tuple(item for il in range(4) for item in (("flip_part", 3, il, 3), ("flip_out", 3, il)))
-    + (("amax", 3, 0), ("amax", 3, 1), ("cast", 3, 1), ("amax", 3, 2), ("cast", 3, 0), ("amax", 3, 3), ("cast", 3, 3), ("cast", 3, 2))
+    (("flip", KL - 1, 0), ("mult", LAST - 3), ("sig_r", LAST - 1), ("add", LAST - 1), ("mm_r", LAST), ("ev_r", LAST), ("mm_z", LAST),
+     ("ev_z", LAST), ("mm_n", LAST - 1), ("tanh", LAST - 2), ("sig_r", LAST), ("ev_n", LAST - 1), ("blend", LAST - 2),
+     ("sig_z", LAST - 1), ("flip", KL - 1, 1), ("mm_n", LAST), ("tanh", LAST - 1), ("ev_n", LAST), ("add", LAST),
+     ("blend", LAST - 1), ("amax", KL - 1, 0))
+    + tuple(("flip_part", KL, il, t) for t in (0, 1) for il in range(2))
+    + (("tanh", LAST), ("sig_z", LAST), ("cast", KL - 1, 0), ("blend", LAST), ("amax", KL - 1, 1))
+    + tuple(("flip_part", KL, il, 2) for il in range(2))
+    + tuple(item for il in range(2) for item in (("flip_part", KL, il, 3), ("flip_out", KL, il)))
+    + (("cast", KL - 1, 1), ("amax", KL, 0), ("amax", KL, 1), ("cast", KL, 0), ("cast", KL, 1))
 )
-CAST_ON_VECTOR = ((3, 0), (3, 2))
-DRAIN_ON_VECTOR = (("add", 14), ("blend", 14), ("blend", 15))
+CAST_ON_VECTOR = ((KL - 1, 1), (KL, 1))
+DRAIN_ON_VECTOR = (("add", LAST - 1), ("blend", LAST))
 
 
 def chunk(q):
-    return q // NJ, (q % NJ) // 4, q % 4
+    b0, bw, g = GROUPS[q // 4]
+    return slice(b0, b0 + bw), g, q % 4
+
+
+def width(q):
+    return GROUPS[q // 4][1]
+
+
+def row_tile(k, il):
+    return GROUPS[k][0] // P + il
 
 
 def x_on_tensor(gate, q):
@@ -182,14 +195,17 @@ def tile_wavernncell_pa_kernel(tc, x, feat, aux1, h, w_ih, w_hh, b_ih, b_hh, out
                 nc.vector.tensor_copy(out=dst, in_=tb[:, 0:step, lo:hi].rearrange("p s r -> p r s"))
 
         def mm_block(gate, q, part="both"):
-            b, g, t = chunk(q)
+            bs, g, t = chunk(q)
             j = 4 * g + t
-            bs = slice(b * BH, (b + 1) * BH)
             last = 2 if x_on_tensor(gate, q) else 1
-            if part != "mx":
+            if width(q) < BH:
+                both = psum.tile([P, 2, width(q)], F32, name="both", tag="acc", bufs=ACC_BANKS)
+                live[("a_ps", gate, q)] = both[:, 0, :]
+                live[("m_ps", gate, q)] = both[:, 1, :]
+            if part != "mx" and width(q) == BH:
                 a_ps = psum.tile([P, BH], F32, name="a_ps", tag="acc", bufs=ACC_BANKS)
                 live[("a_ps", gate, q)] = a_ps
-            if part != "plain":
+            if part != "plain" and width(q) == BH:
                 m_ps = psum.tile([P, BH], F32, name="m_ps", tag="acc", bufs=ACC_BANKS)
                 live[("m_ps", gate, q)] = m_ps
 
@@ -197,40 +213,47 @@ def tile_wavernncell_pa_kernel(tc, x, feat, aux1, h, w_ih, w_hh, b_ih, b_hh, out
                 nc.tensor.matmul(out=live[("a_ps", gate, q)], lhsT=WiT[:, j, SLOTS.index((gate, v)), :], rhs=(fT, aT, xT)[v][:, bs],
                                  start=(v == 0), stop=(v == last))
 
-            if part != "mx":
-                plain(0)
-            if part != "plain":
+            def mx_pair():
                 for c in range(2):
                     w = widx(gate, j)
                     nc.tensor.matmul_mx(out=live[("m_ps", gate, q)], lhsT=wC[:, w, c * P:(c + 1) * P].bitcast(FP8X4),
                                         lhsT_scale=wS[:, w, c * P:(c + 1) * P], rhs=hC[:, c, bs].bitcast(FP8X4),
                                         rhs_scale=hS[:, c, bs], start=(c == 0), stop=(c == 1))
-            if part != "mx":
-                for v in range(1, last + 1):
+
+            if width(q) < BH:
+                if gate != N:
+                    mx_pair()
+                for v in range(last + 1):
                     plain(v)
+                if gate == N:
+                    mx_pair()
+            else:
+                if part != "mx":
+                    plain(0)
+                if part != "plain":
+                    mx_pair()
+                if part != "mx":
+                    for v in range(1, last + 1):
+                        plain(v)
 
         def ev_gate(gate, q, part="both"):
-            b, g, t = chunk(q)
-            bs = slice(b * BH, (b + 1) * BH)
+            bs, g, t = chunk(q)
             if gate == R and part != "mx":
-                a_new = work.tile([P, 2, BH], F32, name="pre_a", tag="pre_a", bufs=2)
+                a_new = work.tile([P, 2, width(q)], F32, name="pre_a", tag="pre_a", bufs=2)
                 live[("pre_a", q)] = a_new
             if gate == R and part != "plain":
-                b_new = work.tile([P, 2, BH], F32, name="pre_b", tag="pre_b", bufs=2)
+                b_new = work.tile([P, 2, width(q)], F32, name="pre_b", tag="pre_b", bufs=2)
                 live[("pre_b", q)] = b_new
             if x_on_tensor(gate, q):
                 pre_a = live[("pre_a", q)][:, gate, :]
                 nc.scalar.copy(out=pre_a, in_=live[("a_ps", gate, q)])
                 nc.vector.tensor_tensor(out=pre_a, in0=pre_a, in1=live[("m_ps", gate, q)], op=ALU.add)
             else:
-                if part != "plain":
-                    nc.vector.scalar_tensor_tensor(out=live[("pre_b", q)][:, gate, :], in0=Xb[:, 1, bs],
-                                                   scalar=wxs[:, 2 * gate + g, t, 1:2], in1=live[("m_ps", gate, q)],
-                                                   op0=ALU.mult, op1=ALU.add)
-                if part != "mx":
-                    nc.vector.scalar_tensor_tensor(out=live[("pre_a", q)][:, gate, :], in0=Xb[:, 0, bs],
-                                                   scalar=wxs[:, 2 * gate + g, t, 0:1], in1=live[("a_ps", gate, q)],
-                                                   op0=ALU.mult, op1=ALU.add)
+                for d in ((1, 0) if width(q) == BH else (0, 1)):
+                    if part != ("mx", "plain")[d]:
+                        nc.vector.scalar_tensor_tensor(out=live[(("pre_a", "pre_b")[d], q)][:, gate, :], in0=Xb[:, d, bs],
+                                                       scalar=wxs[:, 2 * gate + g, t, d:d + 1],
+                                                       in1=live[(("a_ps", "m_ps")[d], gate, q)], op0=ALU.mult, op1=ALU.add)
 
         def add_rz(q, eng):
             pre_a = live[("pre_a", q)]
@@ -239,35 +262,35 @@ def tile_wavernncell_pa_kernel(tc, x, feat, aux1, h, w_ih, w_hh, b_ih, b_hh, out
                 eng.tensor_tensor(out=pre_a[:, gate, :], in0=pre_a[:, gate, :], in1=pre_b[:, gate, :], op=ALU.add)
 
         def sig_gate(gate, q):
-            b, g, t = chunk(q)
+            bs, g, t = chunk(q)
             if gate == R:
-                rz_new = work.tile([P, 2, BH], F32, name="rz", tag="rz", bufs=4)
+                rz_new = work.tile([P, 2, width(q)], F32, name="rz", tag="rz", bufs=4)
                 live[("rz", q)] = rz_new
             nc.scalar.activation(out=live[("rz", q)][:, gate, :], in_=live[("pre_a", q)][:, gate, :], func=ACT.Sigmoid,
                                  bias=bsum[:, 2 * gate + g, t:t + 1], scale=1.0)
 
         def ev_n(q):
-            b, g, t = chunk(q)
-            u = work.tile([P, BH], F32, name="u", tag="u", bufs=2)
+            bs, g, t = chunk(q)
+            u = work.tile([P, width(q)], F32, name="u", tag="u", bufs=2)
             live[("u", q)] = u
             nc.vector.scalar_tensor_tensor(out=u, in0=live[("m_ps", N, q)], scalar=bhf[:, 4 + g, t:t + 1],
                                            in1=live[("rz", q)][:, R, :], op0=ALU.add, op1=ALU.mult)
             nc.vector.tensor_tensor(out=u, in0=u, in1=live[("a_ps", N, q)], op=ALU.add)
 
         def tanh_n(q):
-            b, g, t = chunk(q)
+            bs, g, t = chunk(q)
             if t == 0:
-                n_new = work.tile([P, 4, BH], F32, name="n_grp", tag="n_grp", bufs=2)
+                n_new = work.tile([P, 4, width(q)], F32, name="n_grp", tag="n_grp", bufs=2)
                 live[("n_grp", q // 4)] = n_new
             nc.scalar.activation(out=live[("n_grp", q // 4)][:, t, :], in_=live[("u", q)], func=ACT.Tanh,
                                  bias=bif[:, 4 + g, t:t + 1], scale=1.0)
 
         def blend_sub(q, eng):
-            b, g, t = chunk(q)
+            bs, g, t = chunk(q)
             if t == 0:
-                e_new = work.tile([P, 4, BH], F32, name="e_grp", tag="e_grp", bufs=2)
+                e_new = work.tile([P, 4, width(q)], F32, name="e_grp", tag="e_grp", bufs=2)
                 live[("e_grp", q // 4)] = e_new
-            eng.tensor_tensor(out=live[("e_grp", q // 4)][:, t, :], in0=hGv[:, g, b * BH:(b + 1) * BH, t],
+            eng.tensor_tensor(out=live[("e_grp", q // 4)][:, t, :], in0=hGv[:, g, bs, t],
                               in1=live[("n_grp", q // 4)][:, t, :], op=ALU.subtract)
 
         def blend_mult(q, eng):
@@ -276,16 +299,15 @@ def tile_wavernncell_pa_kernel(tc, x, feat, aux1, h, w_ih, w_hh, b_ih, b_hh, out
 
         def flip_part(k, il, t):
             if t == 0:
-                fl_new = psum.tile([P, 4, P], F32, name="fl", tag="tp" if (k < 3 or il < TP_BANKS) else "acc",
-                                   bufs=TP_BANKS if (k < 3 or il < TP_BANKS) else ACC_BANKS)
+                fl_new = psum.tile([P, 4, P], F32, name="fl", tag="tp", bufs=TP_BANKS)
                 live[("fl", k, il)] = fl_new
             for step, src in enumerate((live[("n_grp", k)], live[("e_grp", k)])):
                 nc.tensor.matmul(out=live[("fl", k, il)][:, t, :], lhsT=src[:, t, il * P:(il + 1) * P], rhs=ident_f,
                                  is_transpose=True, start=(step == 0), stop=(step == 1))
 
         def flip_out(k, il):
-            g = k % 2
-            i = 4 * (k // 2) + il
+            g = GROUPS[k][2]
+            i = row_tile(k, il)
             if g == 0:
                 o_new = work.tile([P, H], F32, name="o_row", tag="o_row", bufs=4)
                 live[("o_row", i)] = o_new
@@ -299,8 +321,8 @@ def tile_wavernncell_pa_kernel(tc, x, feat, aux1, h, w_ih, w_hh, b_ih, b_hh, out
             flip_out(k, il)
 
         def amax(k, il):
-            g = k % 2
-            i = 4 * (k // 2) + il
+            g = GROUPS[k][2]
+            i = row_tile(k, il)
             nc.vector.tensor_reduce(out=am[:, i, g:g + 1], in_=live[("o_row", i)][:, g * 512:(g + 1) * 512], axis=AX.X,
                                     op=ALU.max, apply_absolute_value=True)
             if g == 1:
@@ -309,8 +331,8 @@ def tile_wavernncell_pa_kernel(tc, x, feat, aux1, h, w_ih, w_hh, b_ih, b_hh, out
                 nc.vector.reciprocal(out=sc[:, i:i + 1], in_=sq[:, i:i + 1])
 
         def cast(k, il):
-            i = 4 * (k // 2) + il
-            if k % 2 == 1:
+            i = row_tile(k, il)
+            if GROUPS[k][2] == 1:
                 f8 = work.tile([P, H], FP8, name="f8", tag="f8", bufs=4)
                 if (k, il) in CAST_ON_VECTOR:
                     nc.vector.tensor_scalar(out=f8, in0=live[("o_row", i)], scalar1=sc[:, i:i + 1], scalar2=None,
@@ -478,11 +500,11 @@ def tile_wavernncell_pa_kernel(tc, x, feat, aux1, h, w_ih, w_hh, b_ih, b_hh, out
                 elif name == "amax":
                     move("amax", "cast", 4, amax)
                 elif name == "cast":
-                    move("cast", "", 4, cast)
+                    move("cast", "", 4 if it < 12 else 1, cast)
                 elif 0 <= it - lag:
                     chunk_stage(name, it - lag)
                     if name == "mult" and (it - lag) % 4 == 3:
-                        queue["wait"] = queue["wait"] + [((it - lag) // 4, il, it + FLIP_LAG) for il in range(4)]
+                        queue["wait"] = queue["wait"] + [((it - lag) // 4, il, it + (FLIP_LAG if it < 12 else 2)) for il in range(width(it - lag) // P)]
             prefetch(it)
 
         for item in DRAIN:

@@ -313,7 +313,7 @@ def tile_wavernncell_pa_kernel(tc, x, feat, aux1, h, w_ih, w_hh, b_ih, b_hh, out
                 live[("o_row", i)] = o_new
             dst = live[("o_row", i)][:, g * 512:(g + 1) * 512]
             nc.scalar.copy(out=dst.rearrange("r (p t) -> r p t", t=4), in_=live[("fl", k, il)].rearrange("r t p -> r p t"))
-            nc.scalar.dma_start(out=out_0[i * P:(i + 1) * P, g * 512:(g + 1) * 512], in_=dst)
+            nc.sync.dma_start(out=out_0[i * P:(i + 1) * P, g * 512:(g + 1) * 512], in_=dst)
 
         def flip(k, il):
             for t in range(4):

@@ -33,8 +33,8 @@ PREP = {"prep_a": 2, "prep_b": 0, "prep_c": 3}
 FIRST_EXTRA = 3
 FLIP_LAG = 1
 HOIST = 2
-ORDER = (("add", 1), ("cast", 0), ("prep_b", 0), ("mm_r", 0), ("amax", 0), ("ev_r", 0), ("prep_a", 0), ("tanh", 2), ("quant", 0),
-         ("sig", 1), ("mm_z", 0), ("flip", 0), ("ev_z", 0), ("quant", 0), ("mult", 3), ("sub", 2), ("prep_c", 0), ("mm_n", 1), ("ev_n", 1))
+ORDER = (("add", 1), ("prep_b", 0), ("mm_r", 0), ("amax", 0), ("ev_r", 0), ("prep_a", 0), ("tanh", 2), ("quant", 0),
+         ("sig", 1), ("cast", 0), ("mm_z", 0), ("flip", 0), ("ev_z", 0), ("quant", 0), ("mult", 3), ("sub", 2), ("prep_c", 0), ("mm_n", 1), ("ev_n", 1))
 DRAIN = (
     (("flip", KL - 1, 0), ("mult", LAST - 3), ("sig_r", LAST - 1), ("add", LAST - 1), ("mm_r", LAST), ("ev_r", LAST), ("mm_z", LAST),
      ("ev_z", LAST), ("mm_n", LAST - 1), ("tanh", LAST - 2), ("sig_r", LAST), ("ev_n", LAST - 1), ("blend", LAST - 2),

from contextlib import ExitStack

import concourse.mybir as mybir
from concourse.masks import make_identity

B, H, FEAT, AUX, NS = 1024, 1024, 128, 128, 2
IN = FEAT + AUX + NS
FLOPS = 2 * B * 3 * H * (H + IN)

F32 = mybir.dt.float32
BF16 = mybir.dt.bfloat16
U32 = mybir.dt.uint32
U8 = mybir.dt.uint8
FP8X4 = mybir.dt.float8_e4m3fn_x4
FP8 = mybir.dt.float8_e4m3fn
ALU = mybir.AluOpType
ACT = mybir.ActivationFunctionType
AX = mybir.AxisListType

P = 128
BH = 512
GROUPS = ((0, 512, 0), (0, 512, 1), (512, 512, 0), (512, 256, 1), (768, 256, 1))
NJ = 8
NQ = 4 * len(GROUPS)
LAST = NQ - 1
KL = len(GROUPS) - 1
R, Z, N = 0, 1, 2
ACC_BANKS = 5
TP_BANKS = 3
SLOTS = ((R, 0), (R, 1), (Z, 0), (Z, 1), (R, 2), (N, 0), (N, 1), (N, 2))
COL0 = (0, FEAT, IN - P)
PREP = {"prep_a": 2, "prep_b": 0, "prep_c": 3}
FIRST_EXTRA = 3
FLIP_LAG = 1
HOIST = 2
ORDER = (("add", 1), ("prep_b", 0), ("mm_r", 0), ("amax", 0), ("ev_r", 0), ("prep_a", 0), ("tanh", 2), ("quant", 0),
         ("sig", 1), ("cast", 0), ("mm_z", 0), ("flip", 0), ("ev_z", 0), ("quant", 0), ("mult", 3), ("sub", 2), ("prep_c", 0), ("mm_n", 1), ("ev_n", 1))
DRAIN = (
    (("flip", KL - 1, 0), ("mult", LAST - 3), ("sig_r", LAST - 1), ("add", LAST - 1), ("mm_r", LAST), ("ev_r", LAST), ("mm_z", LAST),
     ("ev_z", LAST), ("mm_n", LAST - 1), ("tanh", LAST - 2), ("sig_r", LAST), ("ev_n", LAST - 1), ("blend", LAST - 2),
     ("sig_z", LAST - 1), ("flip", KL - 1, 1), ("mm_n", LAST), ("tanh", LAST - 1), ("ev_n", LAST), ("add", LAST),
     ("blend", LAST - 1), ("amax", KL - 1, 0))
    + tuple(("flip_part", KL, il, t) for t in (0, 1) for il in range(2))
    + (("tanh", LAST), ("sig_z", LAST), ("cast", KL - 1, 0), ("blend", LAST), ("amax", KL - 1, 1))
    + tuple(("flip_part", KL, il, 2) for il in range(2))
    + tuple(item for il in range(2) for item in (("flip_part", KL, il, 3), ("flip_out", KL, il)))
    + (("cast", KL - 1, 1), ("amax", KL, 0), ("amax", KL, 1), ("cast", KL, 0), ("cast", KL, 1))
)
CAST_ON_VECTOR = ((KL - 1, 1), (KL, 1))
DRAIN_ON_VECTOR = (("add", LAST - 1), ("blend", LAST))


def chunk(q):
    b0, bw, g = GROUPS[q // 4]
    return slice(b0, b0 + bw), g, q % 4


def width(q):
    return GROUPS[q // 4][1]


def row_tile(k, il):
    return GROUPS[k][0] // P + il


def x_on_tensor(gate, q):
    return gate == N or (gate == R and q >= NJ)


def widx(gate, j):
    return 2 * j + gate if gate != N else 2 * NJ + j


def tile_wavernncell_pa_kernel(tc, x, feat, aux1, h, w_ih, w_hh, b_ih, b_hh, out_0, out_1):
    nc = tc.nc
    with ExitStack() as ctx:
        keep = ctx.enter_context(tc.tile_pool(name="keep", bufs=1))
        raw = ctx.enter_context(tc.tile_pool(name="raw", bufs=4))
        work = ctx.enter_context(tc.tile_pool(name="work", bufs=2))
        psum = ctx.enter_context(tc.psum_pool(name="psum", bufs=1))
        ctx.enter_context(tc.manual_schedule())

        ident_f = keep.tile([P, P], F32, name="ident_f")
        ident_b = keep.tile([P, P], BF16, name="ident_b")
        zero = keep.tile([P, 1], F32, name="zero")
        warm = keep.tile([P, 1], F32, name="warm")
        hG = keep.tile([P, 2 * B * 4], BF16, name="hG", align_bytes=64)
        hC = keep.tile([P, 2, B], U32, name="hC", align_bytes=64)
        hS = keep.tile([P, 2, B], U8, name="hS", align_bytes=64)
        wC = keep.tile([P, 3 * NJ, 2 * P], U32, name="wC", align_bytes=64)
        wS = keep.tile([P, 3 * NJ, 2 * P], U8, name="wS", align_bytes=64)
        WiT = keep.tile([P, NJ, len(SLOTS), P], BF16, name="WiT")
        fT = keep.tile([P, B], BF16, name="fT")
        aT = keep.tile([P, B], BF16, name="aT")
        xT = keep.tile([P, B], BF16, name="xT")
        Xb = keep.tile([P, NS, B], BF16, name="Xb")
        wih = keep.tile([P, 6, 4 * IN], BF16, name="wih")
        Xpad = keep.tile([P, 8, P], BF16, name="Xpad")
        fraw = keep.tile([P, 8, FEAT], BF16, name="fraw")
        araw = keep.tile([P, 8, AUX], BF16, name="araw")
        xraw = keep.tile([P, NS * P], BF16, name="xraw")
        braw = keep.tile([P, 4 * P], BF16, name="braw")
        bsum = keep.tile([P, 6, 4], F32, name="bsum")
        bif = keep.tile([P, 6, 4], F32, name="bif")
        bhf = keep.tile([P, 6, 4], F32, name="bhf")
        wxs = keep.tile([P, 6, 4, NS], F32, name="wxs")
        am = keep.tile([P, 8, 2], F32, name="am")
        sq = keep.tile([P, 8], F32, name="sq")
        sc = keep.tile([P, 8], F32, name="sc")

        hG32 = hG.bitcast(F32).rearrange("p (g m u) -> p g m u", g=2, u=2)
        hGv = hG.rearrange("p (g m t) -> p g m t", g=2, t=4)
        wihv = wih.rearrange("p a (t k) -> p a t k", t=4)
        vcopy = nc.vector.tensor_copy
        scopy = nc.scalar.copy
        live = {}

        def load_h(i):
            hr = raw.tile([P, H], BF16, name="hraw", tag="hraw", bufs=4)
            nc.sync.dma_start(out=hr, in_=h[i * P:(i + 1) * P, :])
            live[("hraw", i)] = hr

        def load_w(gate, j):
            g, t = divmod(j, 4)
            r0 = gate * H + g * 512
            wr = raw.tile([P, H], BF16, name="wraw", tag="wraw", bufs=10)
            nc.sync.dma_start(out=wr, in_=w_hh[r0:r0 + 512, :].rearrange("(m t) k -> m t k", t=4)[:, t, :])
            live[("wraw", gate, j)] = wr

        def load_wih(a):
            nc.sync.dma_start(out=wih[:, a, :], in_=w_ih[a * 512:(a + 1) * 512, :].rearrange("(m t) k -> m (t k)", t=4))

        def conv_wx(a):
            nc.vector.tensor_copy(out=wxs[:, a, :, :], in_=wihv[:, a, :, FEAT + AUX:IN])

        def word_transposes(src):
            words = src.bitcast(F32)
            tp = psum.tile([P, 4 * P], F32, name="tp", tag="tp", bufs=TP_BANKS)
            for c in range(2):
                for u in range(2):
                    col = (2 * c + u) * P
                    nc.tensor.transpose(tp[:, col:col + P], words[:, 256 * c + u:256 * (c + 1):2], ident_f)
            return tp.rearrange("p (c u m) -> p c m u", c=2, u=2)

        def prep_h(i, copy):
            copy(out=hG32[:, :, i * P:(i + 1) * P, :], in_=word_transposes(live[("hraw", i)]))

        def quant_h(b):
            for c in range(2):
                col = c * 4 * B + b * 4 * BH
                nc.vector.quantize_mx(out=hC[:, c, b * BH:(b + 1) * BH].bitcast(FP8X4), scales=hS[:, c, b * BH:(b + 1) * BH],
                                      in_=hG[:, col:col + 4 * BH])

        def prep_whh(gate, j, copy):
            k = widx(gate, j)
            if k % 2 == 0:
                wg = work.tile([P, 2, 2 * P * 4], BF16, name="wg", tag="wg", bufs=3, align_bytes=64)
                live[("wg", k // 2)] = wg
            copy(out=live[("wg", k // 2)][:, k % 2, :].bitcast(F32).rearrange("p (c m u) -> p c m u", c=2, u=2),
                 in_=word_transposes(live[("wraw", gate, j)]))

        def quant_whh(pair):
            nc.vector.quantize_mx(out=wC[:, 2 * pair:2 * pair + 2, :].rearrange("p a c -> p (a c)").bitcast(FP8X4),
                                  scales=wS[:, 2 * pair:2 * pair + 2, :].rearrange("p a c -> p (a c)"),
                                  in_=live[("wg", pair)].rearrange("p a c -> p (a c)"))

        def prep_wih(j, lo, hi, copy):
            g, t = divmod(j, 4)
            tb = psum.tile([P, len(SLOTS), P], BF16, name="tb", tag="tp", bufs=TP_BANKS)
            for s in range(lo, hi):
                gate, v = SLOTS[s]
                col = t * IN + COL0[v]
                nc.tensor.transpose(tb[:, s, :], wih[:, 2 * gate + g, col:col + P], ident_b)
            copy(out=WiT[:, j, lo:hi, :], in_=tb[:, lo:hi, :])

        def prep_rows(src, dst, lo, hi, copy):
            tb = psum.tile([P, 8, P], BF16, name="tb", tag="tp", bufs=TP_BANKS)
            for i in range(lo, hi):
                nc.tensor.transpose(tb[:, i, :], src[:, i, :], ident_b)
            copy(out=dst.rearrange("p (i m) -> p i m", i=8)[:, lo:hi, :], in_=tb[:, lo:hi, :])

        def prep_xb(b, copy):
            tb = psum.tile([P, NS, 4, P], BF16, name="tb", tag="tp", bufs=TP_BANKS)
            for d in range(NS):
                for i in range(4):
                    col = P - NS + d
                    nc.tensor.transpose(tb[:, d, i, :], Xpad[:, 4 * b + i, col:col + 1].to_broadcast([P, P]), ident_b)
            copy(out=Xb[:, :, b * BH:(b + 1) * BH], in_=tb.rearrange("p d i m -> p d (i m)"))

        def prep_small(rows, step, outs):
            tb = psum.tile([P, 8, P], BF16, name="tb", tag="tp", bufs=TP_BANKS)
            for s in range(step):
                nc.tensor.transpose(tb[:, s, :], rows[:, s:step * P:step], ident_b)
            for dst, lo, hi in outs:
                nc.vector.tensor_copy(out=dst, in_=tb[:, 0:step, lo:hi].rearrange("p s r -> p r s"))

        def mm_block(gate, q, part="both"):
            bs, g, t = chunk(q)
            j = 4 * g + t
            last = 2 if x_on_tensor(gate, q) else 1
            if width(q) < BH:
                both = psum.tile([P, 2, width(q)], F32, name="both", tag="acc", bufs=ACC_BANKS)
                live[("a_ps", gate, q)] = both[:, 0, :]
                live[("m_ps", gate, q)] = both[:, 1, :]
            if part != "mx" and width(q) == BH:
                a_ps = psum.tile([P, BH], F32, name="a_ps", tag="acc", bufs=ACC_BANKS)
                live[("a_ps", gate, q)] = a_ps
            if part != "plain" and width(q) == BH:
                m_ps = psum.tile([P, BH], F32, name="m_ps", tag="acc", bufs=ACC_BANKS)
                live[("m_ps", gate, q)] = m_ps

            def plain(v):
                nc.tensor.matmul(out=live[("a_ps", gate, q)], lhsT=WiT[:, j, SLOTS.index((gate, v)), :], rhs=(fT, aT, xT)[v][:, bs],
                                 start=(v == 0), stop=(v == last))

            def mx_pair():
                for c in range(2):
                    w = widx(gate, j)
                    nc.tensor.matmul_mx(out=live[("m_ps", gate, q)], lhsT=wC[:, w, c * P:(c + 1) * P].bitcast(FP8X4),
                                        lhsT_scale=wS[:, w, c * P:(c + 1) * P], rhs=hC[:, c, bs].bitcast(FP8X4),
                                        rhs_scale=hS[:, c, bs], start=(c == 0), stop=(c == 1))

            if width(q) < BH:
                if gate != N:
                    mx_pair()
                for v in range(last + 1):
                    plain(v)
                if gate == N:
                    mx_pair()
            else:
                if part != "mx":
                    plain(0)
                if part != "plain":
                    mx_pair()
                if part != "mx":
                    for v in range(1, last + 1):
                        plain(v)

        def ev_gate(gate, q, part="both"):
            bs, g, t = chunk(q)
            if gate == R and part != "mx":
                a_new = work.tile([P, 2, width(q)], F32, name="pre_a", tag="pre_a", bufs=2)
                live[("pre_a", q)] = a_new
            if gate == R and part != "plain":
                b_new = work.tile([P, 2, width(q)], F32, name="pre_b", tag="pre_b", bufs=2)
                live[("pre_b", q)] = b_new
            if x_on_tensor(gate, q):
                pre_a = live[("pre_a", q)][:, gate, :]
                nc.scalar.copy(out=pre_a, in_=live[("a_ps", gate, q)])
                nc.vector.tensor_tensor(out=pre_a, in0=pre_a, in1=live[("m_ps", gate, q)], op=ALU.add)
            else:
                for d in ((1, 0) if width(q) == BH else (0, 1)):
                    if part != ("mx", "plain")[d]:
                        nc.vector.scalar_tensor_tensor(out=live[(("pre_a", "pre_b")[d], q)][:, gate, :], in0=Xb[:, d, bs],
                                                       scalar=wxs[:, 2 * gate + g, t, d:d + 1],
                                                       in1=live[(("a_ps", "m_ps")[d], gate, q)], op0=ALU.mult, op1=ALU.add)

        def add_rz(q, eng):
            pre_a = live[("pre_a", q)]
            pre_b = live[("pre_b", q)]
            for gate in ((Z,) if x_on_tensor(R, q) else (R, Z)):
                eng.tensor_tensor(out=pre_a[:, gate, :], in0=pre_a[:, gate, :], in1=pre_b[:, gate, :], op=ALU.add)

        def sig_gate(gate, q):
            bs, g, t = chunk(q)
            if gate == R:
                rz_new = work.tile([P, 2, width(q)], F32, name="rz", tag="rz", bufs=4)
                live[("rz", q)] = rz_new
            nc.scalar.activation(out=live[("rz", q)][:, gate, :], in_=live[("pre_a", q)][:, gate, :], func=ACT.Sigmoid,
                                 bias=bsum[:, 2 * gate + g, t:t + 1], scale=1.0)

        def ev_n(q):
            bs, g, t = chunk(q)
            u = work.tile([P, width(q)], F32, name="u", tag="u", bufs=2)
            live[("u", q)] = u
            nc.vector.scalar_tensor_tensor(out=u, in0=live[("m_ps", N, q)], scalar=bhf[:, 4 + g, t:t + 1],
                                           in1=live[("rz", q)][:, R, :], op0=ALU.add, op1=ALU.mult)
            nc.vector.tensor_tensor(out=u, in0=u, in1=live[("a_ps", N, q)], op=ALU.add)

        def tanh_n(q):
            bs, g, t = chunk(q)
            if t == 0:
                n_new = work.tile([P, 4, width(q)], F32, name="n_grp", tag="n_grp", bufs=2)
                live[("n_grp", q // 4)] = n_new
            nc.scalar.activation(out=live[("n_grp", q // 4)][:, t, :], in_=live[("u", q)], func=ACT.Tanh,
                                 bias=bif[:, 4 + g, t:t + 1], scale=1.0)

        def blend_sub(q, eng):
            bs, g, t = chunk(q)
            if t == 0:
                e_new = work.tile([P, 4, width(q)], F32, name="e_grp", tag="e_grp", bufs=2)
                live[("e_grp", q // 4)] = e_new
            eng.tensor_tensor(out=live[("e_grp", q // 4)][:, t, :], in0=hGv[:, g, bs, t],
                              in1=live[("n_grp", q // 4)][:, t, :], op=ALU.subtract)

        def blend_mult(q, eng):
            e = live[("e_grp", q // 4)][:, q % 4, :]
            eng.tensor_tensor(out=e, in0=live[("rz", q)][:, Z, :], in1=e, op=ALU.mult)

        def flip_part(k, il, t):
            if t == 0:
                fl_new = psum.tile([P, 4, P], F32, name="fl", tag="tp", bufs=TP_BANKS)
                live[("fl", k, il)] = fl_new
            for step, src in enumerate((live[("n_grp", k)], live[("e_grp", k)])):
                nc.tensor.matmul(out=live[("fl", k, il)][:, t, :], lhsT=src[:, t, il * P:(il + 1) * P], rhs=ident_f,
                                 is_transpose=True, start=(step == 0), stop=(step == 1))

        def flip_out(k, il):
            g = GROUPS[k][2]
            i = row_tile(k, il)
            if g == 0:
                o_new = work.tile([P, H], F32, name="o_row", tag="o_row", bufs=4)
                live[("o_row", i)] = o_new
            dst = live[("o_row", i)][:, g * 512:(g + 1) * 512]
            nc.scalar.copy(out=dst.rearrange("r (p t) -> r p t", t=4), in_=live[("fl", k, il)].rearrange("r t p -> r p t"))
            nc.sync.dma_start(out=out_0[i * P:(i + 1) * P, g * 512:(g + 1) * 512], in_=dst)

        def flip(k, il):
            for t in range(4):
                flip_part(k, il, t)
            flip_out(k, il)

        def amax(k, il):
            g = GROUPS[k][2]
            i = row_tile(k, il)
            nc.vector.tensor_reduce(out=am[:, i, g:g + 1], in_=live[("o_row", i)][:, g * 512:(g + 1) * 512], axis=AX.X,
                                    op=ALU.max, apply_absolute_value=True)
            if g == 1:
                nc.vector.tensor_scalar(out=sq[:, i:i + 1], in0=am[:, i, 0:1], scalar1=am[:, i, 1:2],
                                        scalar2=1.0 / 448.0, op0=ALU.max, op1=ALU.mult)
                nc.vector.reciprocal(out=sc[:, i:i + 1], in_=sq[:, i:i + 1])

        def cast(k, il):
            i = row_tile(k, il)
            if GROUPS[k][2] == 1:
                f8 = work.tile([P, H], FP8, name="f8", tag="f8", bufs=4)
                if (k, il) in CAST_ON_VECTOR:
                    nc.vector.tensor_scalar(out=f8, in0=live[("o_row", i)], scalar1=sc[:, i:i + 1], scalar2=None,
                                            op0=ALU.mult, saturate=False)
                else:
                    nc.scalar.activation(out=f8, in_=live[("o_row", i)], func=ACT.Identity, scale=sc[:, i:i + 1],
                                         bias=zero[:, 0:1], saturate=False)
                nc.sync.dma_start(out=out_1[i * P:(i + 1) * P, :], in_=f8.bitcast(U8))

        fsrc = feat.rearrange("(i m) k -> m i k", m=P)
        asrc = aux1.rearrange("(i m) k -> m i k", m=P)
        nc.vector.memset(xraw, 0.0)
        nc.scalar.dma_start(out=xraw[0:8, :], in_=x.rearrange("(i m) j -> i (m j)", m=P))
        nc.vector.memset(zero, 0.0)
        nc.scalar.activation(out=warm, in_=zero, func=ACT.Sigmoid)
        nc.vector.memset(Xpad, 0.0)
        nc.vector.memset(braw, 0.0)
        make_identity(nc, ident_b)
        make_identity(nc, ident_f)

        nc.sync.dma_start(out=fraw[:, 0:4, :], in_=fsrc[:, 0:4, :])
        nc.sync.dma_start(out=araw[:, 0:4, :], in_=asrc[:, 0:4, :])
        load_wih(0)
        load_wih(2)
        for i in range(4):
            load_h(i)
        load_w(R, 0)
        load_w(Z, 0)
        load_w(N, 0)
        load_wih(4)
        nc.sync.dma_start(out=braw[0:6, :], in_=b_ih.rearrange("(a c) -> a c", a=6))
        nc.sync.dma_start(out=braw[6:12, :], in_=b_hh.rearrange("(a c) -> a c", a=6))
        for j in range(1, 3):
            for gate in (R, Z, N):
                load_w(gate, j)
            if j == 1:
                nc.sync.dma_start(out=fraw[:, 4:8, :], in_=fsrc[:, 4:8, :])
                nc.sync.dma_start(out=araw[:, 4:8, :], in_=asrc[:, 4:8, :])

        prep_rows(fraw, fT, 0, 4, scopy)
        prep_rows(araw, aT, 0, 4, vcopy)
        for q in range(HOIST):
            prep_wih(q, 0, 4, scopy)
        prep_small(xraw, NS, [(Xpad[:, :, P - NS:P], 0, 8)])
        prep_xb(0, vcopy)
        conv_wx(0)
        conv_wx(2)
        for i in range(4):
            prep_h(i, scopy)
            mm_block((R, Z)[i % 2], i // 2, "plain")
            ev_gate((R, Z)[i % 2], i // 2, "plain")
        quant_h(0)
        prep_whh(R, 0, scopy)
        prep_whh(Z, 0, scopy)
        quant_whh(0)

        units = [("whh", N, 0), ("wih", 0, 4), ("x",)]
        for j in range(1, NJ):
            units.extend([("whh", R, j), ("whh", Z, j), ("wih", j, 4 if j < HOIST else 0), ("whh", N, j)])
            if j == 4:
                units.extend([("f",), ("a",), ("xb",)])
            if j >= 4:
                units.append(("h", j))
        queue = {"units": units, "quant": [], "wait": [], "flip": [], "amax": [], "cast": []}

        def do_units(count, share):
            for c, un in enumerate(queue["units"][:count]):
                copy = vcopy if (share and c % 2) else scopy
                if un[0] == "whh":
                    prep_whh(un[1], un[2], copy)
                    if widx(un[1], un[2]) % 2 == 1:
                        queue["quant"].append(widx(un[1], un[2]) // 2)
                elif un[0] == "wih":
                    prep_wih(un[1], un[2], len(SLOTS), copy)
                elif un[0] == "x":
                    prep_rows(Xpad, xT, 0, 8, copy)
                elif un[0] == "f":
                    prep_rows(fraw, fT, 4, 8, copy)
                elif un[0] == "a":
                    prep_rows(araw, aT, 4, 8, copy)
                elif un[0] == "xb":
                    prep_xb(1, copy)
                else:
                    prep_h(un[1], copy)
                    if un[1] == 7:
                        queue["quant"].append(-1)
            queue["units"] = queue["units"][count:]

        def do_quants():
            for pair in queue["quant"]:
                if pair >= 0:
                    quant_whh(pair)
                else:
                    quant_h(1)
            queue["quant"] = []

        def move(src, dst, count, fn):
            for un in queue[src][:count]:
                fn(un[0], un[1])
            if dst:
                queue[dst] = queue[dst] + queue[src][:count]
            queue[src] = queue[src][count:]

        def prefetch(it):
            if it + 3 < NJ:
                for gate in (R, Z, N):
                    load_w(gate, it + 3)
            if it < 4:
                load_h(4 + it)
            if it == 0:
                for gate in (R, Z, N):
                    load_wih(2 * gate + 1)
            if it == 1:
                for gate in (R, Z, N):
                    conv_wx(2 * gate + 1)

        def chunk_stage(name, q):
            eng = nc.vector if (name, q) in DRAIN_ON_VECTOR else nc.gpsimd
            part = "mx" if q < HOIST else "both"
            if name == "mm_r":
                mm_block(R, q, part)
            elif name == "mm_z":
                mm_block(Z, q, part)
            elif name == "mm_n":
                mm_block(N, q)
            elif name == "ev_r":
                ev_gate(R, q, part)
            elif name == "ev_z":
                ev_gate(Z, q, part)
            elif name == "add":
                add_rz(q, eng)
            elif name == "sig":
                sig_gate(R, q)
                sig_gate(Z, q)
            elif name == "sig_r":
                sig_gate(R, q)
            elif name == "sig_z":
                sig_gate(Z, q)
            elif name == "ev_n":
                ev_n(q)
            elif name == "tanh":
                tanh_n(q)
            elif name == "sub":
                blend_sub(q, eng)
            elif name == "mult":
                blend_mult(q, eng)
            else:
                blend_sub(q, eng)
                blend_mult(q, eng)

        for it in range(NQ - 1):
            for name, lag in ORDER:
                if name == "quant":
                    do_quants()
                elif name in PREP:
                    do_units(PREP[name] + (FIRST_EXTRA if it == 0 and name == "prep_b" else 0), it == 0)
                    if it == 0 and name == "prep_b":
                        conv_wx(4)
                        prep_small(braw, 4, [(bif, 0, 6), (bhf, 6, 12)])
                        nc.vector.tensor_tensor(out=bsum, in0=bif, in1=bhf, op=ALU.add)
                elif name == "flip":
                    queue["flip"] = queue["flip"] + [un for un in queue["wait"] if un[2] <= it]
                    queue["wait"] = [un for un in queue["wait"] if un[2] > it]
                    move("flip", "amax", 1 if it < NJ else 2, flip)
                elif name == "amax":
                    move("amax", "cast", 4, amax)
                elif name == "cast":
                    move("cast", "", 4 if it < 12 else 1, cast)
                elif 0 <= it - lag:
                    chunk_stage(name, it - lag)
                    if name == "mult" and (it - lag) % 4 == 3:
                        queue["wait"] = queue["wait"] + [((it - lag) // 4, il, it + (FLIP_LAG if it < 12 else 2)) for il in range(width(it - lag) // P)]
            prefetch(it)

        for item in DRAIN:
            if item[0] == "flip":
                flip(item[1], item[2])
            elif item[0] == "flip_part":
                flip_part(item[1], item[2], item[3])
            elif item[0] == "flip_out":
                flip_out(item[1], item[2])
            elif item[0] == "amax":
                amax(item[1], item[2])
            elif item[0] == "cast":
                cast(item[1], item[2])
            else:
                chunk_stage(item[0], item[1])
